import numpy as np
import ml_dtypes


def mxq(x, axis, fmt="e4m3"):
    dtype, down = {"e4m3": (ml_dtypes.float8_e4m3fn, 7), "e5m2": (ml_dtypes.float8_e5m2, 14)}[fmt]
    v = np.moveaxis(np.asarray(x, np.float32).astype(ml_dtypes.bfloat16).astype(np.float64), axis, -1)
    blocks = v.reshape(v.shape[:-1] + (-1, 32))
    amax = np.abs(blocks).max(-1, keepdims=True)
    byte = np.maximum(np.where(amax > 0, np.frexp(amax)[1] - 1 + 127, 0) - down, 1)
    scale = np.exp2(byte - 127.0)
    codes = (blocks / scale).astype(np.float32).astype(dtype).astype(np.float64)
    return np.moveaxis((codes * scale).reshape(v.shape), -1, axis)


WIDE = False


def mx_kscale(k):
    if not WIDE:
        return np.ones(k)
    levels = np.array([10, -10, 5, -5, 0])
    a = np.random.permutation(np.resize(levels, k // 512 * 4)).reshape(k // 512, 4)
    idx = np.arange(k)
    return np.exp2(a[idx // 512, idx % 128 // 32])


BF16 = ml_dtypes.bfloat16


def bf(x):
    return np.asarray(x, np.float32).astype(BF16)


def f64(x):
    return np.asarray(x).astype(np.float64)


B, S, K, IN, HID, OUT = 4, 32, 16, 1024, 512, 511
LN_EPS = 1e-5
LINK_EPS = 1e-8


def sigmoid(v):
    return 1.0 / (1.0 + np.exp(-v))


def setup_inputs():
    s, t = mx_kscale(IN), mx_kscale(HID)
    keep = np.random.random((B, S, 1, 1)) > 0.125
    return {"net_in": bf(np.random.standard_normal((B, S, K, IN)) * s),
            "embeds": bf(np.random.standard_normal((B, S, OUT)) * 0.5),
            "m": bf(np.random.random((B, S, K, 1)) * keep),
            "W1": bf(np.random.standard_normal((IN, HID)) / np.sqrt(IN) / s[:, None] * t),
            "b1": bf(np.random.standard_normal(HID) * 0.3 * t),
            "Wf": bf(np.random.standard_normal((HID, OUT + 1)) * 3.0 / np.sqrt(HID) / t[:, None]),
            "b_f": bf(np.random.standard_normal(OUT + 1) * 0.3),
            "gamma": bf(1.0 + 0.1 * np.random.standard_normal(OUT)),
            "beta": bf(0.1 * np.random.standard_normal(OUT))}


def reference(net_in, embeds, m, W1, b1, Wf, b_f, gamma, beta):
    h = np.maximum((mxq(f64(net_in), 3, "e4m3") @ mxq(f64(W1), 0, "e4m3")) + f64(b1), 0.0)
    out = (mxq(h, 3, "e4m3") @ mxq(f64(Wf), 0, "e4m3")) + f64(b_f)
    out = np.concatenate([out[..., :-1], sigmoid(out[..., -1:])], axis=-1)
    out = f64(m) * out
    link_weight = out[..., -1] + LINK_EPS
    norm = link_weight.sum(axis=2, keepdims=True)
    weights = (link_weight / norm)[..., None]
    updates = (out * weights).sum(axis=2)
    upd_weights = updates[..., -1:]
    embeds_new = f64(embeds) + upd_weights * updates[..., :-1]
    mu = embeds_new.mean(axis=-1, keepdims=True)
    var = ((embeds_new - mu) ** 2).mean(axis=-1, keepdims=True)
    return (embeds_new - mu) / np.sqrt(var + LN_EPS) * f64(gamma) + f64(beta)

@@ -1,0 +1,281 @@
+from contextlib import ExitStack
+
+import concourse.masks as masks
+import concourse.mybir as mybir
+
+F32 = mybir.dt.float32
+BF16 = mybir.dt.bfloat16
+U32 = mybir.dt.uint32
+U8 = mybir.dt.uint8
+I32 = mybir.dt.int32
+FP8X4 = mybir.dt.float8_e4m3fn_x4
+ACT = mybir.ActivationFunctionType
+ALU = mybir.AluOpType
+AX = mybir.AxisListType
+
+P = 128
+TOK = 128
+LINKS = 16
+IN = 1024
+HID = 512
+CH = 512
+OUT = 511
+LN_EPS = 1e-5
+LINK_EPS = 1e-8
+GROUPS = [2, 2, 2, 2, 2, 2, 2, 2]
+NG = len(GROUPS)
+LEAD_A = 4
+LEAD_B = 2
+BANKS = {"x": 2, "h": 2, "o": 4}
+PINNED = True
+
+FLOPS = 2 * TOK * LINKS * IN * HID + 2 * TOK * LINKS * HID * CH
+
+
+def tile_embed_update_pa_kernel(tc, net_in, embeds, m, W1, b1, Wf, b_f, gamma, beta, out):
+    nc = tc.nc
+    x2d = net_in.rearrange("b s k i -> (b s) (k i)")
+    m2d = m.rearrange("b s k o -> (b s) (k o)")
+    emb2d = embeds.rearrange("b s c -> (b s) c")
+    out2d = out.rearrange("b s c -> (b s) c")
+    w1v = W1.rearrange("(g u p e) c -> g p u (e c)", g=2, u=2, p=P, e=2)
+    wfv = Wf.rearrange("(t p) c -> p t c", t=4, p=P)
+
+    with ExitStack() as ctx:
+        keep = ctx.enter_context(tc.tile_pool(name="keep", bufs=1))
+        psx = ctx.enter_context(tc.psum_pool(name="psx", bufs=BANKS["x"]))
+        psh = ctx.enter_context(tc.psum_pool(name="psh", bufs=BANKS["h"]))
+        pso = ctx.enter_context(tc.psum_pool(name="pso", bufs=BANKS["o"]))
+        if PINNED:
+            ctx.enter_context(tc.manual_schedule())
+
+        ident = keep.tile([P, P], F32, name="ident")
+        masks.make_identity(nc, ident[:])
+        vecs = keep.tile([P, 3 * CH], BF16, name="vecs")
+        nc.vector.memset(vecs[:].bitcast(I32), 0)
+        ones = keep.tile([P, P], BF16, name="ones")
+        nc.vector.memset(ones[:], 1.0)
+        epsln = keep.tile([P, 1], F32, name="epsln")
+        nc.vector.memset(epsln[:], LN_EPS)
+
+        scr = keep.tile([P, 1], F32, name="scr")
+        nc.scalar.activation(out=scr[:], in_=epsln[:], func=ACT.Sigmoid)
+        mbf = keep.tile([P, LINKS], BF16, name="mbf")
+        w1r = [keep.tile([P, 4, HID], BF16, name="w1r%d" % g) for g in range(2)]
+        wfr = keep.tile([P, 4, CH], BF16, name="wfr")
+        xr = [keep.tile([P, 2 * IN], BF16, name="xr%d" % c) for c in range(LINKS // 2)]
+        b1t = keep.tile([P, 4], BF16, name="b1t")
+        emb = keep.tile([P, OUT], BF16, name="emb")
+
+        def load_w1(g):
+            nc.sync.dma_start(out=w1r[g][:].rearrange("p (u e) c -> p u (e c)", u=2, e=2), in_=w1v[g])
+
+        def load_x(c):
+            nc.sync.dma_start(out=xr[c][:], in_=x2d[:, c * 2 * IN:(c + 1) * 2 * IN])
+
+        load_w1(0)
+        load_x(0)
+        nc.sync.dma_start(out=vecs[0:1, 0:CH], in_=b_f.unsqueeze(0))
+        nc.sync.dma_start(out=mbf[:], in_=m2d)
+        with nc.allow_non_contiguous_dma(reason="512 bias values, one to a partition and chunk"):
+            nc.sync.dma_start(out=b1t[:], in_=b1.rearrange("(j p) -> p j", p=P))
+        load_w1(1)
+        load_x(1)
+        nc.sync.dma_start(out=wfr[:], in_=wfv)
+        for c in range(2, LINKS // 2):
+            load_x(c)
+        nc.sync.dma_start(out=emb[:], in_=emb2d)
+        nc.sync.dma_start(out=vecs[0:1, CH:CH + OUT], in_=gamma.unsqueeze(0))
+        nc.sync.dma_start(out=vecs[0:1, 2 * CH:2 * CH + OUT], in_=beta.unsqueeze(0))
+
+        b1f = keep.tile([P, 4], F32, name="b1f")
+        mf = keep.tile([P, LINKS], F32, name="mf")
+        msq = keep.tile([P, LINKS], F32, name="msq")
+        mep = keep.tile([P, LINKS], F32, name="mep")
+        bgate = keep.tile([P, 1], F32, name="bgate")
+        w1c = keep.tile([P, 2 * HID], U32, name="w1c", align_bytes=64)
+        w1s = keep.tile([P, 2 * HID], U8, name="w1s", align_bytes=64)
+        w1g = [keep.tile([P, HID, 4], BF16, name="w1g%d" % g, align_bytes=64) for g in range(2)]
+        wfc = keep.tile([P, CH], U32, name="wfc", align_bytes=64)
+        wfs = keep.tile([P, CH], U8, name="wfs", align_bytes=64)
+        wfg = keep.tile([P, CH, 4], BF16, name="wfg", align_bytes=64)
+        first = [sum(GROUPS[:i]) for i in range(len(GROUPS))]
+        xg, xc, xs, hpl, hgr, hc, hs = [], [], [], [], [], [], []
+        for G, n in enumerate(GROUPS):
+            xg.append(keep.tile([P, 2 * n * TOK * 4], BF16, name="xg%d" % G, align_bytes=64))
+            xc.append(keep.tile([P, 2 * n * TOK], U32, name="xc%d" % G, align_bytes=64))
+            xs.append(keep.tile([P, 2 * n * TOK], U8, name="xs%d" % G, align_bytes=64))
+            hpl.append(keep.tile([P, 4, n * TOK], BF16, name="hpl%d" % G))
+            hgr.append(keep.tile([P, n * TOK, 4], BF16, name="hgr%d" % G, align_bytes=64))
+            hc.append(keep.tile([P, n * TOK], U32, name="hc%d" % G, align_bytes=64))
+            hs.append(keep.tile([P, n * TOK], U8, name="hs%d" % G, align_bytes=64))
+        sg = keep.tile([P, LINKS], F32, name="sg")
+        st = keep.tile([P, 3, LINKS], F32, name="st")
+        acc = keep.tile([P, CH], F32, name="acc")
+        banks = {}
+
+        def regroup(copy, dst, src):
+            copy(out=dst.rearrange("p (c i) t -> p c t i", i=4),
+                 in_=src.rearrange("p t (c i) -> p c t i", i=4))
+
+        def quantise(codes, scales, grouped):
+            nc.vector.quantize_mx(out=codes.bitcast(FP8X4), scales=scales, in_=grouped)
+
+        def small_prep():
+            nc.vector.tensor_copy(out=b1f[:], in_=b1t[:])
+            nc.vector.tensor_copy(out=mf[:], in_=mbf[:])
+            nc.vector.tensor_tensor(out=msq[:], in0=mf[:], in1=mf[:], op=ALU.mult)
+            nc.vector.tensor_scalar(out=mep[:], in0=mf[:], scalar1=LINK_EPS, scalar2=None, op0=ALU.mult)
+
+        def gate_bias():
+            bf0 = pso.tile([P, CH], F32, name="bfp0", tag="ops")
+            nc.tensor.matmul(out=bf0[:], lhsT=ones[:], rhs=vecs[:, 0:CH], start=True, stop=True)
+            nc.vector.tensor_copy(out=bgate[:], in_=bf0[:, OUT:CH])
+
+        def prep_w1(g):
+            regroup(nc.vector.tensor_copy, w1g[g][:], w1r[g][:])
+            quantise(w1c[:, g * HID:(g + 1) * HID], w1s[:, g * HID:(g + 1) * HID],
+                     w1g[g][:].rearrange("p c t -> p (c t)"))
+
+        def prep_wf():
+            regroup(nc.vector.tensor_copy, wfg[:], wfr[:])
+            quantise(wfc[:], wfs[:], wfg[:].rearrange("p c t -> p (c t)"))
+
+        def transposes(k):
+            words = xr[k // 2][:].bitcast(F32)
+            xt = psx.tile([P, 4, TOK], F32, name="xt", tag="xt")
+            banks["x%d" % k] = xt
+            for w in range(4):
+                lo = (k % 2) * (IN // 2) + w * P
+                nc.tensor.transpose(out=xt[:, w, :], in_=words[:, lo:lo + P], identity=ident[:])
+
+        def x_exit(G, l):
+            n = GROUPS[G]
+            dst = xg[G][:].bitcast(F32).rearrange("p (g l t u) -> p g l t u", g=2, l=n, t=TOK, u=2)
+            xt = banks["x%d" % (first[G] + l)]
+            nc.scalar.copy(out=dst[:, :, l, :, :], in_=xt[:].rearrange("p (g u) t -> p g t u", g=2, u=2))
+
+        def stage1(G, b):
+            n = GROUPS[G]
+            w = n * TOK
+            per = 4 // n
+            hp = psh.tile([P, per, w], F32, name="hp", tag="hp")
+            banks["h%d_%d" % (G, b)] = hp
+            for jj in range(per):
+                j = b * per + jj
+                for g in range(2):
+                    lo = g * HID + j * P
+                    nc.tensor.matmul_mx(out=hp[:, jj, :],
+                                        lhsT=w1c[:, lo:lo + P].bitcast(FP8X4), lhsT_scale=w1s[:, lo:lo + P],
+                                        rhs=xc[G][:, g * w:(g + 1) * w].bitcast(FP8X4),
+                                        rhs_scale=xs[G][:, g * w:(g + 1) * w],
+                                        start=(g == 0), stop=(g == 1))
+
+        def h_exit(G, j):
+            per = 4 // GROUPS[G]
+            hp = banks["h%d_%d" % (G, j // per)]
+            nc.scalar.activation(out=hpl[G][:, j, :], in_=hp[:, j % per, :], func=ACT.Relu,
+                                 bias=b1f[:, j:j + 1], scale=1.0)
+
+        def stage2(G, l):
+            op = pso.tile([P, CH], F32, name="op", tag="ops")
+            banks["o%d" % (first[G] + l)] = op
+            nc.tensor.matmul_mx(out=op[:],
+                                lhsT=hc[G][:, l * TOK:(l + 1) * TOK].bitcast(FP8X4),
+                                lhsT_scale=hs[G][:, l * TOK:(l + 1) * TOK],
+                                rhs=wfc[:].bitcast(FP8X4), rhs_scale=wfs[:], start=True, stop=True)
+
+        def gate(k):
+            nc.scalar.activation(out=sg[:, k:k + 1], in_=banks["o%d" % k][:, OUT:CH], func=ACT.Sigmoid,
+                                 bias=bgate[:, 0:1], scale=1.0)
+
+        def weight(k):
+            nc.scalar.activation(out=st[:, 2, k:k + 1], in_=sg[:, k:k + 1], func=ACT.Identity,
+                                 bias=mep[:, k:k + 1], scale=msq[:, k:k + 1])
+
+        def pool_link(k):
+            op = banks["o%d" % k]
+            if k == 0:
+                nc.vector.tensor_scalar(out=acc[:, 0:OUT], in0=op[:, 0:OUT],
+                                        scalar1=st[:, 2, k:k + 1], scalar2=None, op0=ALU.mult)
+            else:
+                nc.vector.scalar_tensor_tensor(out=acc[:, 0:OUT], in0=op[:, 0:OUT],
+                                               scalar=st[:, 2, k:k + 1], in1=acc[:, 0:OUT],
+                                               op0=ALU.mult, op1=ALU.add)
+
+        for i in range(-LEAD_A, NG):
+            ga, gb, gc = i + LEAD_A, i + LEAD_B, i
+            has_a, has_b, has_c = ga < NG, 0 <= gb < NG, gc >= 0
+            if i == -LEAD_A:
+                prep_w1(0)
+                small_prep()
+                prep_w1(1)
+            if has_c:
+                for l in range(GROUPS[gc]):
+                    stage2(gc, l)
+                for l in range(GROUPS[gc]):
+                    gate(first[gc] + l)
+                    weight(first[gc] + l)
+            if has_b:
+                for b in range(GROUPS[gb]):
+                    stage1(gb, b)
+                for j in range(4):
+                    h_exit(gb, j)
+            if has_c:
+                pool_link(first[gc])
+            if has_b:
+                regroup(nc.vector.tensor_copy, hgr[gb][:], hpl[gb][:])
+            if has_c:
+                pool_link(first[gc] + 1)
+            if has_b:
+                quantise(hc[gb][:], hs[gb][:], hgr[gb][:].rearrange("p r j -> p (r j)"))
+            if has_a:
+                for l in range(GROUPS[ga]):
+                    transposes(first[ga] + l)
+                for l in range(GROUPS[ga]):
+                    x_exit(ga, l)
+                quantise(xc[ga][:], xs[ga][:], xg[ga][:])
+            if i == 1 - LEAD_A:
+                gate_bias()
+                prep_wf()
+
+        nc.scalar.activation(out=scr[:], in_=sg[:, LINKS - 1:LINKS], func=ACT.Abs_reciprocal_sqrt,
+                             bias=epsln[:, 0:1], scale=1.0)
+        gam = psx.tile([P, CH], F32, name="gam", tag="xt")
+        nc.tensor.matmul(out=gam[:], lhsT=ones[:], rhs=vecs[:, CH:2 * CH], start=True, stop=True)
+        bet = psx.tile([P, CH], F32, name="bet", tag="xt")
+        nc.tensor.matmul(out=bet[:], lhsT=ones[:], rhs=vecs[:, 2 * CH:3 * CH], start=True, stop=True)
+        bfp = psh.tile([P, CH], F32, name="bfp", tag="hp")
+        nc.tensor.matmul(out=bfp[:], lhsT=ones[:], rhs=vecs[:, 0:CH], start=True, stop=True)
+
+        gg = keep.tile([P, LINKS], F32, name="gg")
+        nc.vector.tensor_tensor(out=gg[:], in0=sg[:], in1=mf[:], op=ALU.mult)
+        nc.vector.tensor_scalar(out=st[:, 0, :], in0=gg[:], scalar1=LINK_EPS, scalar2=None, op0=ALU.add)
+        nc.vector.tensor_tensor(out=st[:, 1, :], in0=st[:, 0, :], in1=gg[:], op=ALU.mult)
+        sums = keep.tile([P, 3], F32, name="sums")
+        nc.vector.tensor_reduce(out=sums[:], in_=st[:], axis=AX.X, op=ALU.add)
+        rl = keep.tile([P, 1], F32, name="rl")
+        nc.vector.reciprocal(out=rl[:], in_=sums[:, 0:1])
+        sc = keep.tile([P, 1], F32, name="sc")
+        nc.vector.tensor_scalar(out=sc[:], in0=sums[:, 1:2], scalar1=rl[:, 0:1], scalar2=rl[:, 0:1],
+                                op0=ALU.mult, op1=ALU.mult)
+        u1 = keep.tile([P, CH], F32, name="u1")
+        nc.vector.scalar_tensor_tensor(out=u1[:, 0:OUT], in0=bfp[:, 0:OUT], scalar=sums[:, 2:3],
+                                       in1=acc[:, 0:OUT], op0=ALU.mult, op1=ALU.add)
+        ee = keep.tile([P, CH], F32, name="ee")
+        nc.vector.scalar_tensor_tensor(out=ee[:, 0:OUT], in0=u1[:, 0:OUT], scalar=sc[:, 0:1],
+                                       in1=emb[:], op0=ALU.mult, op1=ALU.add)
+        bst = keep.tile([P, 6], F32, name="bst")
+        nc.vector.bn_stats(out=bst[:], in_=ee[:, 0:OUT])
+        mv = keep.tile([P, 2], F32, name="mv")
+        nc.vector.bn_aggr(out=mv[:], in_=bst[:])
+        rstd = keep.tile([P, 1], F32, name="rstd")
+        nc.scalar.activation(out=rstd[:], in_=mv[:, 1:2], func=ACT.Abs_reciprocal_sqrt,
+                             bias=epsln[:, 0:1], scale=1.0)
+        y1 = keep.tile([P, CH], F32, name="y1")
+        nc.vector.scalar_tensor_tensor(out=y1[:, 0:OUT], in0=ee[:, 0:OUT], scalar=mv[:, 0:1],
+                                       in1=gam[:, 0:OUT], op0=ALU.subtract, op1=ALU.mult)
+        yy = keep.tile([P, CH], F32, name="yy")
+        nc.vector.scalar_tensor_tensor(out=yy[:, 0:OUT], in0=y1[:, 0:OUT], scalar=rstd[:, 0:1],
+                                       in1=bet[:, 0:OUT], op0=ALU.mult, op1=ALU.add)
+        nc.sync.dma_start(out=out2d, in_=yy[:, 0:OUT])

@@ -75,12 +75,12 @@ def tile_embed_update_pa_kernel(tc, net_in, embeds, m, W1, b1, Wf, b_f, gamma, b
 
         load_w1(0)
         load_x(0)
-        nc.sync.dma_start(out=vecs[0:1, 0:CH], in_=b_f.unsqueeze(0))
-        nc.sync.dma_start(out=mbf[:], in_=m2d)
-        with nc.allow_non_contiguous_dma(reason="512 bias values, one to a partition and chunk"):
-            nc.sync.dma_start(out=b1t[:], in_=b1.rearrange("(j p) -> p j", p=P))
         load_w1(1)
         load_x(1)
+        with nc.allow_non_contiguous_dma(reason="512 bias values, one to a partition and chunk"):
+            nc.sync.dma_start(out=b1t[:], in_=b1.rearrange("(j p) -> p j", p=P))
+        nc.sync.dma_start(out=vecs[0:1, 0:CH], in_=b_f.unsqueeze(0))
+        nc.sync.dma_start(out=mbf[:], in_=m2d)
         nc.sync.dma_start(out=wfr[:], in_=wfv)
         for c in range(2, LINKS // 2):
             load_x(c)
@@ -112,6 +112,8 @@ def tile_embed_update_pa_kernel(tc, net_in, embeds, m, W1, b1, Wf, b_f, gamma, b
         sg = keep.tile([P, LINKS], F32, name="sg")
         st = keep.tile([P, 3, LINKS], F32, name="st")
         acc = keep.tile([P, CH], F32, name="acc")
+        gg = keep.tile([P, LINKS], F32, name="gg")
+        sums = keep.tile([P, 3], F32, name="sums")
         banks = {}
 
         def regroup(copy, dst, src):
@@ -132,14 +134,9 @@ def tile_embed_update_pa_kernel(tc, net_in, embeds, m, W1, b1, Wf, b_f, gamma, b
             nc.tensor.matmul(out=bf0[:], lhsT=ones[:], rhs=vecs[:, 0:CH], start=True, stop=True)
             nc.vector.tensor_copy(out=bgate[:], in_=bf0[:, OUT:CH])
 
-        def prep_w1(g):
-            regroup(nc.vector.tensor_copy, w1g[g][:], w1r[g][:])
+        def quantise_w1(g):
             quantise(w1c[:, g * HID:(g + 1) * HID], w1s[:, g * HID:(g + 1) * HID],
                      w1g[g][:].rearrange("p c t -> p (c t)"))
-
-        def prep_wf():
-            regroup(nc.vector.tensor_copy, wfg[:], wfr[:])
-            quantise(wfc[:], wfs[:], wfg[:].rearrange("p c t -> p (c t)"))
 
         def transposes(k):
             words = xr[k // 2][:].bitcast(F32)
@@ -206,25 +203,35 @@ def tile_embed_update_pa_kernel(tc, net_in, embeds, m, W1, b1, Wf, b_f, gamma, b
         for i in range(-LEAD_A, NG):
             ga, gb, gc = i + LEAD_A, i + LEAD_B, i
             has_a, has_b, has_c = ga < NG, 0 <= gb < NG, gc >= 0
+            last = i == NG - 1
             if i == -LEAD_A:
-                prep_w1(0)
+                regroup(nc.vector.tensor_copy, w1g[0][:], w1r[0][:])
+                quantise_w1(0)
+                regroup(nc.vector.tensor_copy, w1g[1][:], w1r[1][:])
+            if i == 1 - LEAD_A:
                 small_prep()
-                prep_w1(1)
+                regroup(nc.vector.tensor_copy, wfg[:], wfr[:])
             if has_c:
                 for l in range(GROUPS[gc]):
                     stage2(gc, l)
                 for l in range(GROUPS[gc]):
                     gate(first[gc] + l)
+                for l in range(GROUPS[gc]):
                     weight(first[gc] + l)
             if has_b:
                 for b in range(GROUPS[gb]):
                     stage1(gb, b)
                 for j in range(4):
                     h_exit(gb, j)
+            if last:
+                nc.vector.tensor_tensor(out=gg[:], in0=sg[:], in1=mf[:], op=ALU.mult)
+                nc.vector.tensor_reduce(out=sums[:, 2:3], in_=st[:, 2, :], axis=AX.X, op=ALU.add)
             if has_c:
                 pool_link(first[gc])
             if has_b:
                 regroup(nc.vector.tensor_copy, hgr[gb][:], hpl[gb][:])
+            if last:
+                nc.vector.tensor_scalar(out=st[:, 0, :], in0=gg[:], scalar1=LINK_EPS, scalar2=None, op0=ALU.add)
             if has_c:
                 pool_link(first[gc] + 1)
             if has_b:
@@ -235,9 +242,11 @@ def tile_embed_update_pa_kernel(tc, net_in, embeds, m, W1, b1, Wf, b_f, gamma, b
                 for l in range(GROUPS[ga]):
                     x_exit(ga, l)
                 quantise(xc[ga][:], xs[ga][:], xg[ga][:])
+            if i == -LEAD_A:
+                quantise_w1(1)
             if i == 1 - LEAD_A:
                 gate_bias()
-                prep_wf()
+                quantise(wfc[:], wfs[:], wfg[:].rearrange("p c t -> p (c t)"))
 
         nc.scalar.activation(out=scr[:], in_=sg[:, LINKS - 1:LINKS], func=ACT.Abs_reciprocal_sqrt,
                              bias=epsln[:, 0:1], scale=1.0)
@@ -248,34 +257,39 @@ def tile_embed_update_pa_kernel(tc, net_in, embeds, m, W1, b1, Wf, b_f, gamma, b
         bfp = psh.tile([P, CH], F32, name="bfp", tag="hp")
         nc.tensor.matmul(out=bfp[:], lhsT=ones[:], rhs=vecs[:, 0:CH], start=True, stop=True)
 
-        gg = keep.tile([P, LINKS], F32, name="gg")
-        nc.vector.tensor_tensor(out=gg[:], in0=sg[:], in1=mf[:], op=ALU.mult)
-        nc.vector.tensor_scalar(out=st[:, 0, :], in0=gg[:], scalar1=LINK_EPS, scalar2=None, op0=ALU.add)
-        nc.vector.tensor_tensor(out=st[:, 1, :], in0=st[:, 0, :], in1=gg[:], op=ALU.mult)
-        sums = keep.tile([P, 3], F32, name="sums")
-        nc.vector.tensor_reduce(out=sums[:], in_=st[:], axis=AX.X, op=ALU.add)
+        halves = [(0, 256), (256, OUT)]
         rl = keep.tile([P, 1], F32, name="rl")
-        nc.vector.reciprocal(out=rl[:], in_=sums[:, 0:1])
         sc = keep.tile([P, 1], F32, name="sc")
+        ee = keep.tile([P, CH], F32, name="ee")
+        bst = keep.tile([P, 2, 6], F32, name="bst")
+        mv = keep.tile([P, 2], F32, name="mv")
+        rstd = keep.tile([P, 1], F32, name="rstd")
+        y1 = keep.tile([P, CH], F32, name="y1")
+        yy = keep.tile([P, CH], F32, name="yy")
+
+        def add_bias(lo, hi):
+            nc.vector.scalar_tensor_tensor(out=acc[:, lo:hi], in0=bfp[:, lo:hi], scalar=sums[:, 2:3],
+                                           in1=acc[:, lo:hi], op0=ALU.mult, op1=ALU.add)
+
+        nc.vector.tensor_tensor(out=st[:, 1, :], in0=st[:, 0, :], in1=gg[:], op=ALU.mult)
+        add_bias(0, 256)
+        nc.vector.tensor_reduce(out=sums[:, 0:2], in_=st[:, 0:2, :], axis=AX.X, op=ALU.add)
+        add_bias(256, OUT)
+        nc.vector.reciprocal(out=rl[:], in_=sums[:, 0:1])
         nc.vector.tensor_scalar(out=sc[:], in0=sums[:, 1:2], scalar1=rl[:, 0:1], scalar2=rl[:, 0:1],
                                 op0=ALU.mult, op1=ALU.mult)
-        u1 = keep.tile([P, CH], F32, name="u1")
-        nc.vector.scalar_tensor_tensor(out=u1[:, 0:OUT], in0=bfp[:, 0:OUT], scalar=sums[:, 2:3],
-                                       in1=acc[:, 0:OUT], op0=ALU.mult, op1=ALU.add)
-        ee = keep.tile([P, CH], F32, name="ee")
-        nc.vector.scalar_tensor_tensor(out=ee[:, 0:OUT], in0=u1[:, 0:OUT], scalar=sc[:, 0:1],
-                                       in1=emb[:], op0=ALU.mult, op1=ALU.add)
-        bst = keep.tile([P, 6], F32, name="bst")
-        nc.vector.bn_stats(out=bst[:], in_=ee[:, 0:OUT])
-        mv = keep.tile([P, 2], F32, name="mv")
-        nc.vector.bn_aggr(out=mv[:], in_=bst[:])
-        rstd = keep.tile([P, 1], F32, name="rstd")
+        for lo, hi in halves:
+            nc.vector.scalar_tensor_tensor(out=ee[:, lo:hi], in0=acc[:, lo:hi], scalar=sc[:, 0:1],
+                                           in1=emb[:, lo:hi], op0=ALU.mult, op1=ALU.add)
+        for h, (lo, hi) in enumerate(halves):
+            nc.vector.bn_stats(out=bst[:, h, :], in_=ee[:, lo:hi])
+        nc.vector.bn_aggr(out=mv[:], in_=bst[:].rearrange("p h s -> p (h s)"))
         nc.scalar.activation(out=rstd[:], in_=mv[:, 1:2], func=ACT.Abs_reciprocal_sqrt,
                              bias=epsln[:, 0:1], scale=1.0)
-        y1 = keep.tile([P, CH], F32, name="y1")
-        nc.vector.scalar_tensor_tensor(out=y1[:, 0:OUT], in0=ee[:, 0:OUT], scalar=mv[:, 0:1],
-                                       in1=gam[:, 0:OUT], op0=ALU.subtract, op1=ALU.mult)
-        yy = keep.tile([P, CH], F32, name="yy")
-        nc.vector.scalar_tensor_tensor(out=yy[:, 0:OUT], in0=y1[:, 0:OUT], scalar=rstd[:, 0:1],
-                                       in1=bet[:, 0:OUT], op0=ALU.mult, op1=ALU.add)
-        nc.sync.dma_start(out=out2d, in_=yy[:, 0:OUT])
+        for lo, hi in halves:
+            nc.vector.scalar_tensor_tensor(out=y1[:, lo:hi], in0=ee[:, lo:hi], scalar=mv[:, 0:1],
+                                           in1=gam[:, lo:hi], op0=ALU.subtract, op1=ALU.mult)
+        for lo, hi in halves:
+            nc.vector.scalar_tensor_tensor(out=yy[:, lo:hi], in0=y1[:, lo:hi], scalar=rstd[:, 0:1],
+                                           in1=bet[:, lo:hi], op0=ALU.mult, op1=ALU.add)
+            nc.sync.dma_start(out=out2d[:, lo:hi], in_=yy[:, lo:hi])

@@ -81,10 +81,10 @@ def tile_embed_update_pa_kernel(tc, net_in, embeds, m, W1, b1, Wf, b_f, gamma, b
             nc.sync.dma_start(out=b1t[:], in_=b1.rearrange("(j p) -> p j", p=P))
         nc.sync.dma_start(out=vecs[0:1, 0:CH], in_=b_f.unsqueeze(0))
         nc.sync.dma_start(out=mbf[:], in_=m2d)
+        nc.sync.dma_start(out=emb[:], in_=emb2d)
         nc.sync.dma_start(out=wfr[:], in_=wfv)
         for c in range(2, LINKS // 2):
             load_x(c)
-        nc.sync.dma_start(out=emb[:], in_=emb2d)
         nc.sync.dma_start(out=vecs[0:1, CH:CH + OUT], in_=gamma.unsqueeze(0))
         nc.sync.dma_start(out=vecs[0:1, 2 * CH:2 * CH + OUT], in_=beta.unsqueeze(0))
 
@@ -190,7 +190,7 @@ def tile_embed_update_pa_kernel(tc, net_in, embeds, m, W1, b1, Wf, b_f, gamma, b
             nc.scalar.activation(out=st[:, 2, k:k + 1], in_=sg[:, k:k + 1], func=ACT.Identity,
                                  bias=mep[:, k:k + 1], scale=msq[:, k:k + 1])
 
-        def pool_link(k):
+        def pool_link(k, total=None):
             op = banks["o%d" % k]
             if k == 0:
                 nc.vector.tensor_scalar(out=acc[:, 0:OUT], in0=op[:, 0:OUT],
@@ -198,7 +198,15 @@ def tile_embed_update_pa_kernel(tc, net_in, embeds, m, W1, b1, Wf, b_f, gamma, b
             else:
                 nc.vector.scalar_tensor_tensor(out=acc[:, 0:OUT], in0=op[:, 0:OUT],
                                                scalar=st[:, 2, k:k + 1], in1=acc[:, 0:OUT],
-                                               op0=ALU.mult, op1=ALU.add)
+                                               op0=ALU.mult, op1=ALU.add, accum_out=total)
+
+        sacc = keep.tile([P, 1], F32, name="sacc")
+        nes = keep.tile([P, 1], F32, name="nes")
+        scr2 = keep.tile([P, CH], F32, name="scr2")
+        lgt = keep.tile([P, LINKS], F32, name="lgt")
+        rl = keep.tile([P, 1], F32, name="rl")
+        sc = keep.tile([P, 1], F32, name="sc")
+        nsc = keep.tile([P, 1], F32, name="nsc")
 
         for i in range(-LEAD_A, NG):
             ga, gb, gc = i + LEAD_A, i + LEAD_B, i
@@ -226,14 +234,26 @@ def tile_embed_update_pa_kernel(tc, net_in, embeds, m, W1, b1, Wf, b_f, gamma, b
             if last:
                 nc.vector.tensor_tensor(out=gg[:], in0=sg[:], in1=mf[:], op=ALU.mult)
                 nc.vector.tensor_reduce(out=sums[:, 2:3], in_=st[:, 2, :], axis=AX.X, op=ALU.add)
+                bfp = psh.tile([P, CH], F32, name="bfp", tag="hp")
+                nc.tensor.matmul(out=bfp[:], lhsT=ones[:], rhs=vecs[:, 0:CH], start=True, stop=True)
             if has_c:
                 pool_link(first[gc])
             if has_b:
                 regroup(nc.vector.tensor_copy, hgr[gb][:], hpl[gb][:])
             if last:
-                nc.vector.tensor_scalar(out=st[:, 0, :], in0=gg[:], scalar1=LINK_EPS, scalar2=None, op0=ALU.add)
+                nc.vector.scalar_tensor_tensor(out=lgt[:], in0=gg[:], scalar=LINK_EPS, in1=gg[:],
+                                               op0=ALU.add, op1=ALU.mult, accum_out=sums[:, 1:2])
+                nc.vector.tensor_scalar(out=st[:, 0, :], in0=gg[:], scalar1=LINK_EPS, scalar2=None, op0=ALU.add,
+                                        op1=ALU.add, accum_out=sums[:, 0:1])
+                nc.vector.scalar_tensor_tensor(out=acc[:, 0:OUT], in0=bfp[:, 0:OUT], scalar=sums[:, 2:3],
+                                               in1=acc[:, 0:OUT], op0=ALU.mult, op1=ALU.add)
+                nc.vector.reciprocal(out=rl[:], in_=sums[:, 0:1])
+                nc.vector.tensor_scalar(out=sc[:], in0=sums[:, 1:2], scalar1=rl[:, 0:1], scalar2=rl[:, 0:1],
+                                        op0=ALU.mult, op1=ALU.mult)
             if has_c:
-                pool_link(first[gc] + 1)
+                pool_link(first[gc] + 1, total=sacc[:, 0:1] if last else None)
+            if last:
+                nc.vector.tensor_scalar(out=nsc[:], in0=sc[:], scalar1=-1.0 / OUT, scalar2=None, op0=ALU.mult)
             if has_b:
                 quantise(hc[gb][:], hs[gb][:], hgr[gb][:].rearrange("p r j -> p (r j)"))
             if has_a:
@@ -245,6 +265,8 @@ def tile_embed_update_pa_kernel(tc, net_in, embeds, m, W1, b1, Wf, b_f, gamma, b
             if i == -LEAD_A:
                 quantise_w1(1)
             if i == 1 - LEAD_A:
+                nc.scalar.activation(out=scr2[:, 0:OUT], in_=emb[:], func=ACT.Copy, scale=-1.0 / OUT,
+                                     accum_out=nes[:, 0:1])
                 gate_bias()
                 quantise(wfc[:], wfs[:], wfg[:].rearrange("p c t -> p (c t)"))
 
@@ -254,41 +276,35 @@ def tile_embed_update_pa_kernel(tc, net_in, embeds, m, W1, b1, Wf, b_f, gamma, b
         nc.tensor.matmul(out=gam[:], lhsT=ones[:], rhs=vecs[:, CH:2 * CH], start=True, stop=True)
         bet = psx.tile([P, CH], F32, name="bet", tag="xt")
         nc.tensor.matmul(out=bet[:], lhsT=ones[:], rhs=vecs[:, 2 * CH:3 * CH], start=True, stop=True)
-        bfp = psh.tile([P, CH], F32, name="bfp", tag="hp")
-        nc.tensor.matmul(out=bfp[:], lhsT=ones[:], rhs=vecs[:, 0:CH], start=True, stop=True)
 
         halves = [(0, 256), (256, OUT)]
-        rl = keep.tile([P, 1], F32, name="rl")
-        sc = keep.tile([P, 1], F32, name="sc")
         ee = keep.tile([P, CH], F32, name="ee")
-        bst = keep.tile([P, 2, 6], F32, name="bst")
-        mv = keep.tile([P, 2], F32, name="mv")
+        negmu = keep.tile([P, 1], F32, name="negmu")
+        vs = keep.tile([P, 2], F32, name="vs")
+        vt = keep.tile([P, 1], F32, name="vt")
         rstd = keep.tile([P, 1], F32, name="rstd")
         y1 = keep.tile([P, CH], F32, name="y1")
         yy = keep.tile([P, CH], F32, name="yy")
 
-        def add_bias(lo, hi):
-            nc.vector.scalar_tensor_tensor(out=acc[:, lo:hi], in0=bfp[:, lo:hi], scalar=sums[:, 2:3],
-                                           in1=acc[:, lo:hi], op0=ALU.mult, op1=ALU.add)
-
-        nc.vector.tensor_tensor(out=st[:, 1, :], in0=st[:, 0, :], in1=gg[:], op=ALU.mult)
-        add_bias(0, 256)
-        nc.vector.tensor_reduce(out=sums[:, 0:2], in_=st[:, 0:2, :], axis=AX.X, op=ALU.add)
-        add_bias(256, OUT)
-        nc.vector.reciprocal(out=rl[:], in_=sums[:, 0:1])
-        nc.vector.tensor_scalar(out=sc[:], in0=sums[:, 1:2], scalar1=rl[:, 0:1], scalar2=rl[:, 0:1],
-                                op0=ALU.mult, op1=ALU.mult)
-        for lo, hi in halves:
+        def residual(lo, hi):
             nc.vector.scalar_tensor_tensor(out=ee[:, lo:hi], in0=acc[:, lo:hi], scalar=sc[:, 0:1],
                                            in1=emb[:, lo:hi], op0=ALU.mult, op1=ALU.add)
+
+        residual(*halves[0])
+        nc.vector.tensor_scalar(out=negmu[:], in0=sacc[:], scalar1=nsc[:, 0:1], scalar2=nes[:, 0:1],
+                                op0=ALU.mult, op1=ALU.add)
+        residual(*halves[1])
         for h, (lo, hi) in enumerate(halves):
-            nc.vector.bn_stats(out=bst[:, h, :], in_=ee[:, lo:hi])
-        nc.vector.bn_aggr(out=mv[:], in_=bst[:].rearrange("p h s -> p (h s)"))
-        nc.scalar.activation(out=rstd[:], in_=mv[:, 1:2], func=ACT.Abs_reciprocal_sqrt,
-                             bias=epsln[:, 0:1], scale=1.0)
+            nc.scalar.activation(out=scr2[:, lo:hi], in_=ee[:, lo:hi], func=ACT.Square,
+                                 bias=negmu[:, 0:1], scale=1.0, accum_out=vs[:, h:h + 1])
+            if h == 0:
+                nc.scalar.activation(out=vt[:], in_=vs[:, 0:1], func=ACT.Identity,
+                                     bias=epsln[:, 0:1], scale=1.0 / OUT)
+        nc.scalar.activation(out=rstd[:], in_=vs[:, 1:2], func=ACT.Abs_reciprocal_sqrt,
+                             bias=vt[:, 0:1], scale=1.0 / OUT)
         for lo, hi in halves:
-            nc.vector.scalar_tensor_tensor(out=y1[:, lo:hi], in0=ee[:, lo:hi], scalar=mv[:, 0:1],
-                                           in1=gam[:, lo:hi], op0=ALU.subtract, op1=ALU.mult)
+            nc.vector.scalar_tensor_tensor(out=y1[:, lo:hi], in0=ee[:, lo:hi], scalar=negmu[:, 0:1],
+                                           in1=gam[:, lo:hi], op0=ALU.add, op1=ALU.mult)
         for lo, hi in halves:
             nc.vector.scalar_tensor_tensor(out=yy[:, lo:hi], in0=y1[:, lo:hi], scalar=rstd[:, 0:1],
                                            in1=bet[:, lo:hi], op0=ALU.mult, op1=ALU.add)

@@ -53,7 +53,7 @@ def tile_embed_update_pa_kernel(tc, net_in, embeds, m, W1, b1, Wf, b_f, gamma, b
         masks.make_identity(nc, ident[:])
         vecs = keep.tile([P, 3 * CH], BF16, name="vecs")
         nc.vector.memset(vecs[:].bitcast(I32), 0)
-        ones = keep.tile([P, P], BF16, name="ones")
+        ones = keep.tile([P, CH], BF16, name="ones")
         nc.vector.memset(ones[:], 1.0)
         epsln = keep.tile([P, 1], F32, name="epsln")
         nc.vector.memset(epsln[:], LN_EPS)
@@ -131,12 +131,17 @@ def tile_embed_update_pa_kernel(tc, net_in, embeds, m, W1, b1, Wf, b_f, gamma, b
 
         def gate_bias():
             bf0 = pso.tile([P, CH], F32, name="bfp0", tag="ops")
-            nc.tensor.matmul(out=bf0[:], lhsT=ones[:], rhs=vecs[:, 0:CH], start=True, stop=True)
+            nc.tensor.matmul(out=bf0[:], lhsT=ones[:, 0:P], rhs=vecs[:, 0:CH], start=True, stop=True)
             nc.vector.tensor_copy(out=bgate[:], in_=bf0[:, OUT:CH])
 
         def quantise_w1(g):
             quantise(w1c[:, g * HID:(g + 1) * HID], w1s[:, g * HID:(g + 1) * HID],
                      w1g[g][:].rearrange("p c t -> p (c t)"))
+
+        def warm(count):
+            wb = pso.tile([P, CH], F32, name="warmup", tag="ops")
+            for r in range(count):
+                nc.tensor.matmul(out=wb[:], lhsT=ones[:, 0:P], rhs=ones[:], start=True, stop=True)
 
         def transposes(k):
             words = xr[k // 2][:].bitcast(F32)
@@ -235,7 +240,7 @@ def tile_embed_update_pa_kernel(tc, net_in, embeds, m, W1, b1, Wf, b_f, gamma, b
                 nc.vector.tensor_tensor(out=gg[:], in0=sg[:], in1=mf[:], op=ALU.mult)
                 nc.vector.tensor_reduce(out=sums[:, 2:3], in_=st[:, 2, :], axis=AX.X, op=ALU.add)
                 bfp = psh.tile([P, CH], F32, name="bfp", tag="hp")
-                nc.tensor.matmul(out=bfp[:], lhsT=ones[:], rhs=vecs[:, 0:CH], start=True, stop=True)
+                nc.tensor.matmul(out=bfp[:], lhsT=ones[:, 0:P], rhs=vecs[:, 0:CH], start=True, stop=True)
             if has_c:
                 pool_link(first[gc])
             if has_b:
@@ -256,9 +261,14 @@ def tile_embed_update_pa_kernel(tc, net_in, embeds, m, W1, b1, Wf, b_f, gamma, b
                 nc.vector.tensor_scalar(out=nsc[:], in0=sc[:], scalar1=-1.0 / OUT, scalar2=None, op0=ALU.mult)
             if has_b:
                 quantise(hc[gb][:], hs[gb][:], hgr[gb][:].rearrange("p r j -> p (r j)"))
+            if i == -LEAD_A:
+                warm(5)
             if has_a:
                 for l in range(GROUPS[ga]):
                     transposes(first[ga] + l)
+            if i == -LEAD_A or i == 1 - LEAD_A:
+                warm(3)
+            if has_a:
                 for l in range(GROUPS[ga]):
                     x_exit(ga, l)
                 quantise(xc[ga][:], xs[ga][:], xg[ga][:])
@@ -273,9 +283,9 @@ def tile_embed_update_pa_kernel(tc, net_in, embeds, m, W1, b1, Wf, b_f, gamma, b
         nc.scalar.activation(out=scr[:], in_=sg[:, LINKS - 1:LINKS], func=ACT.Abs_reciprocal_sqrt,
                              bias=epsln[:, 0:1], scale=1.0)
         gam = psx.tile([P, CH], F32, name="gam", tag="xt")
-        nc.tensor.matmul(out=gam[:], lhsT=ones[:], rhs=vecs[:, CH:2 * CH], start=True, stop=True)
+        nc.tensor.matmul(out=gam[:], lhsT=ones[:, 0:P], rhs=vecs[:, CH:2 * CH], start=True, stop=True)
         bet = psx.tile([P, CH], F32, name="bet", tag="xt")
-        nc.tensor.matmul(out=bet[:], lhsT=ones[:], rhs=vecs[:, 2 * CH:3 * CH], start=True, stop=True)
+        nc.tensor.matmul(out=bet[:], lhsT=ones[:, 0:P], rhs=vecs[:, 2 * CH:3 * CH], start=True, stop=True)
 
         halves = [(0, 256), (256, OUT)]
         ee = keep.tile([P, CH], F32, name="ee")

@@ -28,6 +28,8 @@ LEAD_A = 4
 LEAD_B = 2
 BANKS = {"x": 2, "h": 2, "o": 4}
 PINNED = True
+TAIL_SHARE = 128
+GATE_COLS = 64
 
 FLOPS = 2 * TOK * LINKS * IN * HID + 2 * TOK * LINKS * HID * CH
 
@@ -79,10 +81,10 @@ def tile_embed_update_pa_kernel(tc, net_in, embeds, m, W1, b1, Wf, b_f, gamma, b
         load_x(1)
         with nc.allow_non_contiguous_dma(reason="512 bias values, one to a partition and chunk"):
             nc.sync.dma_start(out=b1t[:], in_=b1.rearrange("(j p) -> p j", p=P))
+        nc.sync.dma_start(out=wfr[:], in_=wfv)
         nc.sync.dma_start(out=vecs[0:1, 0:CH], in_=b_f.unsqueeze(0))
         nc.sync.dma_start(out=mbf[:], in_=m2d)
         nc.sync.dma_start(out=emb[:], in_=emb2d)
-        nc.sync.dma_start(out=wfr[:], in_=wfv)
         for c in range(2, LINKS // 2):
             load_x(c)
         nc.sync.dma_start(out=vecs[0:1, CH:CH + OUT], in_=gamma.unsqueeze(0))
@@ -111,6 +113,7 @@ def tile_embed_update_pa_kernel(tc, net_in, embeds, m, W1, b1, Wf, b_f, gamma, b
             hs.append(keep.tile([P, n * TOK], U8, name="hs%d" % G, align_bytes=64))
         sg = keep.tile([P, LINKS], F32, name="sg")
         st = keep.tile([P, 3, LINKS], F32, name="st")
+        wt = keep.tile([P, LINKS], F32, name="wt")
         acc = keep.tile([P, CH], F32, name="acc")
         gg = keep.tile([P, LINKS], F32, name="gg")
         sums = keep.tile([P, 3], F32, name="sums")
@@ -124,10 +127,10 @@ def tile_embed_update_pa_kernel(tc, net_in, embeds, m, W1, b1, Wf, b_f, gamma, b
             nc.vector.quantize_mx(out=codes.bitcast(FP8X4), scales=scales, in_=grouped)
 
         def small_prep():
-            nc.vector.tensor_copy(out=b1f[:], in_=b1t[:])
-            nc.vector.tensor_copy(out=mf[:], in_=mbf[:])
-            nc.vector.tensor_tensor(out=msq[:], in0=mf[:], in1=mf[:], op=ALU.mult)
-            nc.vector.tensor_scalar(out=mep[:], in0=mf[:], scalar1=LINK_EPS, scalar2=None, op0=ALU.mult)
+            nc.gpsimd.tensor_copy(out=b1f[:], in_=b1t[:])
+            nc.gpsimd.tensor_copy(out=mf[:], in_=mbf[:])
+            nc.gpsimd.tensor_tensor(out=msq[:], in0=mf[:], in1=mf[:], op=ALU.mult)
+            nc.gpsimd.tensor_scalar(out=mep[:], in0=mf[:], scalar1=LINK_EPS, scalar2=0.0, op0=ALU.mult, op1=ALU.add)
 
         def gate_bias():
             bf0 = pso.tile([P, CH], F32, name="bfp0", tag="ops")
@@ -191,24 +194,38 @@ def tile_embed_update_pa_kernel(tc, net_in, embeds, m, W1, b1, Wf, b_f, gamma, b
             nc.scalar.activation(out=sg[:, k:k + 1], in_=banks["o%d" % k][:, OUT:CH], func=ACT.Sigmoid,
                                  bias=bgate[:, 0:1], scale=1.0)
 
-        def weight(k):
-            nc.scalar.activation(out=st[:, 2, k:k + 1], in_=sg[:, k:k + 1], func=ACT.Identity,
-                                 bias=mep[:, k:k + 1], scale=msq[:, k:k + 1])
+        def early_gates(G):
+            k, n = first[G], GROUPS[G]
+            gl = psx.tile([P, n, GATE_COLS], F32, name="gl", tag="xt")
+            for l in range(n):
+                nc.tensor.matmul_mx(out=gl[:, l, :],
+                                    lhsT=hc[G][:, l * TOK:(l + 1) * TOK].bitcast(FP8X4),
+                                    lhsT_scale=hs[G][:, l * TOK:(l + 1) * TOK],
+                                    rhs=wfc[:, CH - GATE_COLS:CH].bitcast(FP8X4),
+                                    rhs_scale=wfs[:, CH - GATE_COLS:CH], start=True, stop=True)
+            nc.scalar.activation(out=sg[:, k:k + n], in_=gl[:, :, GATE_COLS - 1], func=ACT.Sigmoid,
+                                 bias=bgate[:, 0:1], scale=1.0)
 
-        def pool_link(k, total=None):
+        def weights(G):
+            k, n = first[G], GROUPS[G]
+            nc.gpsimd.tensor_tensor(out=wt[:, k:k + n], in0=sg[:, k:k + n], in1=msq[:, k:k + n], op=ALU.mult)
+            nc.gpsimd.tensor_tensor(out=st[:, 2, k:k + n], in0=wt[:, k:k + n], in1=mep[:, k:k + n], op=ALU.add)
+
+        def pool_link(k):
             op = banks["o%d" % k]
-            if k == 0:
-                nc.vector.tensor_scalar(out=acc[:, 0:OUT], in0=op[:, 0:OUT],
-                                        scalar1=st[:, 2, k:k + 1], scalar2=None, op0=ALU.mult)
-            else:
-                nc.vector.scalar_tensor_tensor(out=acc[:, 0:OUT], in0=op[:, 0:OUT],
-                                               scalar=st[:, 2, k:k + 1], in1=acc[:, 0:OUT],
-                                               op0=ALU.mult, op1=ALU.add, accum_out=total)
+            for lo, hi in [(0, OUT)] if k < 12 else halves:
+                if k == 0:
+                    nc.vector.tensor_scalar(out=acc[:, lo:hi], in0=op[:, lo:hi],
+                                            scalar1=st[:, 2, k:k + 1], scalar2=None, op0=ALU.mult)
+                else:
+                    nc.vector.scalar_tensor_tensor(out=acc[:, lo:hi], in0=op[:, lo:hi],
+                                                   scalar=st[:, 2, k:k + 1], in1=acc[:, lo:hi],
+                                                   op0=ALU.mult, op1=ALU.add)
 
+        halves = [(0, 256), (256, OUT)]
         sacc = keep.tile([P, 1], F32, name="sacc")
         nes = keep.tile([P, 1], F32, name="nes")
         scr2 = keep.tile([P, CH], F32, name="scr2")
-        lgt = keep.tile([P, LINKS], F32, name="lgt")
         rl = keep.tile([P, 1], F32, name="rl")
         sc = keep.tile([P, 1], F32, name="sc")
         nsc = keep.tile([P, 1], F32, name="nsc")
@@ -227,37 +244,53 @@ def tile_embed_update_pa_kernel(tc, net_in, embeds, m, W1, b1, Wf, b_f, gamma, b
             if has_c:
                 for l in range(GROUPS[gc]):
                     stage2(gc, l)
-                for l in range(GROUPS[gc]):
-                    gate(first[gc] + l)
-                for l in range(GROUPS[gc]):
-                    weight(first[gc] + l)
+                if not last:
+                    for l in range(GROUPS[gc]):
+                        gate(first[gc] + l)
+                    if gc == NG - 2:
+                        for k in range(first[gc], first[gc] + 2):
+                            nc.scalar.activation(out=st[:, 2, k:k + 1], in_=sg[:, k:k + 1], func=ACT.Identity,
+                                                 bias=mep[:, k:k + 1], scale=msq[:, k:k + 1])
+                    else:
+                        weights(gc)
+                if gc == NG - 2:
+                    nc.scalar.activation(out=scr2[:, 0:OUT], in_=emb[:], func=ACT.Copy, scale=-1.0 / OUT,
+                                         accum_out=nes[:, 0:1])
+                    early_gates(NG - 1)
+                    for k in range(first[NG - 1], LINKS):
+                        nc.scalar.activation(out=st[:, 2, k:k + 1], in_=sg[:, k:k + 1], func=ACT.Identity,
+                                             bias=mep[:, k:k + 1], scale=msq[:, k:k + 1])
+                    nc.gpsimd.tensor_tensor(out=gg[:], in0=sg[:], in1=mf[:], op=ALU.mult)
+                    nc.gpsimd.tensor_scalar(out=st[:, 0, :], in0=gg[:], scalar1=LINK_EPS, scalar2=1.0,
+                                            op0=ALU.add, op1=ALU.mult)
+                    nc.gpsimd.tensor_tensor(out=st[:, 1, :], in0=st[:, 0, :], in1=gg[:], op=ALU.mult)
+                    bfp = psh.tile([P, CH], F32, name="bfp", tag="hp")
+                    nc.tensor.matmul(out=bfp[:], lhsT=ones[:, 0:P], rhs=vecs[:, 0:CH], start=True, stop=True)
             if has_b:
                 for b in range(GROUPS[gb]):
                     stage1(gb, b)
                 for j in range(4):
                     h_exit(gb, j)
-            if last:
-                nc.vector.tensor_tensor(out=gg[:], in0=sg[:], in1=mf[:], op=ALU.mult)
-                nc.vector.tensor_reduce(out=sums[:, 2:3], in_=st[:, 2, :], axis=AX.X, op=ALU.add)
-                bfp = psh.tile([P, CH], F32, name="bfp", tag="hp")
-                nc.tensor.matmul(out=bfp[:], lhsT=ones[:, 0:P], rhs=vecs[:, 0:CH], start=True, stop=True)
+                if gb == 0:
+                    gate_bias()
             if has_c:
                 pool_link(first[gc])
             if has_b:
-                regroup(nc.vector.tensor_copy, hgr[gb][:], hpl[gb][:])
+                share = TAIL_SHARE if gb >= NG - 2 else 0
+                w = GROUPS[gb] * TOK
+                if share:
+                    regroup(nc.scalar.copy, hgr[gb][:, w - share:w, :], hpl[gb][:, :, w - share:w])
+                regroup(nc.vector.tensor_copy, hgr[gb][:, 0:w - share, :], hpl[gb][:, :, 0:w - share])
             if last:
-                nc.vector.scalar_tensor_tensor(out=lgt[:], in0=gg[:], scalar=LINK_EPS, in1=gg[:],
-                                               op0=ALU.add, op1=ALU.mult, accum_out=sums[:, 1:2])
-                nc.vector.tensor_scalar(out=st[:, 0, :], in0=gg[:], scalar1=LINK_EPS, scalar2=None, op0=ALU.add,
-                                        op1=ALU.add, accum_out=sums[:, 0:1])
-                nc.vector.scalar_tensor_tensor(out=acc[:, 0:OUT], in0=bfp[:, 0:OUT], scalar=sums[:, 2:3],
-                                               in1=acc[:, 0:OUT], op0=ALU.mult, op1=ALU.add)
+                nc.vector.tensor_reduce(out=sums[:], in_=st[:], axis=AX.X, op=ALU.add)
+            if has_c:
+                pool_link(first[gc] + 1)
+            if last:
                 nc.vector.reciprocal(out=rl[:], in_=sums[:, 0:1])
                 nc.vector.tensor_scalar(out=sc[:], in0=sums[:, 1:2], scalar1=rl[:, 0:1], scalar2=rl[:, 0:1],
                                         op0=ALU.mult, op1=ALU.mult)
-            if has_c:
-                pool_link(first[gc] + 1, total=sacc[:, 0:1] if last else None)
-            if last:
+                nc.vector.scalar_tensor_tensor(out=acc[:, 0:OUT], in0=bfp[:, 0:OUT], scalar=sums[:, 2:3],
+                                               in1=acc[:, 0:OUT], op0=ALU.mult, op1=ALU.add, accum_out=sacc[:, 0:1])
                 nc.vector.tensor_scalar(out=nsc[:], in0=sc[:], scalar1=-1.0 / OUT, scalar2=None, op0=ALU.mult)
             if has_b:
                 quantise(hc[gb][:], hs[gb][:], hgr[gb][:].rearrange("p r j -> p (r j)"))
@@ -267,7 +300,7 @@ def tile_embed_update_pa_kernel(tc, net_in, embeds, m, W1, b1, Wf, b_f, gamma, b
                 for l in range(GROUPS[ga]):
                     transposes(first[ga] + l)
             if i == -LEAD_A or i == 1 - LEAD_A:
-                warm(3)
+                warm(3 if i == -LEAD_A else 1)
             if has_a:
                 for l in range(GROUPS[ga]):
                     x_exit(ga, l)
@@ -275,9 +308,6 @@ def tile_embed_update_pa_kernel(tc, net_in, embeds, m, W1, b1, Wf, b_f, gamma, b
             if i == -LEAD_A:
                 quantise_w1(1)
             if i == 1 - LEAD_A:
-                nc.scalar.activation(out=scr2[:, 0:OUT], in_=emb[:], func=ACT.Copy, scale=-1.0 / OUT,
-                                     accum_out=nes[:, 0:1])
-                gate_bias()
                 quantise(wfc[:], wfs[:], wfg[:].rearrange("p c t -> p (c t)"))
 
         nc.scalar.activation(out=scr[:], in_=sg[:, LINKS - 1:LINKS], func=ACT.Abs_reciprocal_sqrt,
@@ -287,11 +317,9 @@ def tile_embed_update_pa_kernel(tc, net_in, embeds, m, W1, b1, Wf, b_f, gamma, b
         bet = psx.tile([P, CH], F32, name="bet", tag="xt")
         nc.tensor.matmul(out=bet[:], lhsT=ones[:, 0:P], rhs=vecs[:, 2 * CH:3 * CH], start=True, stop=True)
 
-        halves = [(0, 256), (256, OUT)]
         ee = keep.tile([P, CH], F32, name="ee")
         negmu = keep.tile([P, 1], F32, name="negmu")
-        vs = keep.tile([P, 2], F32, name="vs")
-        vt = keep.tile([P, 1], F32, name="vt")
+        vs = keep.tile([P, 1], F32, name="vs")
         rstd = keep.tile([P, 1], F32, name="rstd")
         y1 = keep.tile([P, CH], F32, name="y1")
         yy = keep.tile([P, CH], F32, name="yy")
@@ -304,14 +332,10 @@ def tile_embed_update_pa_kernel(tc, net_in, embeds, m, W1, b1, Wf, b_f, gamma, b
         nc.vector.tensor_scalar(out=negmu[:], in0=sacc[:], scalar1=nsc[:, 0:1], scalar2=nes[:, 0:1],
                                 op0=ALU.mult, op1=ALU.add)
         residual(*halves[1])
-        for h, (lo, hi) in enumerate(halves):
-            nc.scalar.activation(out=scr2[:, lo:hi], in_=ee[:, lo:hi], func=ACT.Square,
-                                 bias=negmu[:, 0:1], scale=1.0, accum_out=vs[:, h:h + 1])
-            if h == 0:
-                nc.scalar.activation(out=vt[:], in_=vs[:, 0:1], func=ACT.Identity,
-                                     bias=epsln[:, 0:1], scale=1.0 / OUT)
-        nc.scalar.activation(out=rstd[:], in_=vs[:, 1:2], func=ACT.Abs_reciprocal_sqrt,
-                             bias=vt[:, 0:1], scale=1.0 / OUT)
+        nc.scalar.activation(out=scr2[:, 0:OUT], in_=ee[:, 0:OUT], func=ACT.Square,
+                             bias=negmu[:, 0:1], scale=1.0, accum_out=vs[:])
+        nc.scalar.activation(out=rstd[:], in_=vs[:], func=ACT.Abs_reciprocal_sqrt,
+                             bias=epsln[:, 0:1], scale=1.0 / OUT)
         for lo, hi in halves:
             nc.vector.scalar_tensor_tensor(out=y1[:, lo:hi], in0=ee[:, lo:hi], scalar=negmu[:, 0:1],
                                            in1=gam[:, lo:hi], op0=ALU.add, op1=ALU.mult)

@@ -113,7 +113,6 @@ def tile_embed_update_pa_kernel(tc, net_in, embeds, m, W1, b1, Wf, b_f, gamma, b
             hs.append(keep.tile([P, n * TOK], U8, name="hs%d" % G, align_bytes=64))
         sg = keep.tile([P, LINKS], F32, name="sg")
         st = keep.tile([P, 3, LINKS], F32, name="st")
-        wt = keep.tile([P, LINKS], F32, name="wt")
         acc = keep.tile([P, CH], F32, name="acc")
         gg = keep.tile([P, LINKS], F32, name="gg")
         sums = keep.tile([P, 3], F32, name="sums")
@@ -127,10 +126,10 @@ def tile_embed_update_pa_kernel(tc, net_in, embeds, m, W1, b1, Wf, b_f, gamma, b
             nc.vector.quantize_mx(out=codes.bitcast(FP8X4), scales=scales, in_=grouped)
 
         def small_prep():
-            nc.gpsimd.tensor_copy(out=b1f[:], in_=b1t[:])
-            nc.gpsimd.tensor_copy(out=mf[:], in_=mbf[:])
-            nc.gpsimd.tensor_tensor(out=msq[:], in0=mf[:], in1=mf[:], op=ALU.mult)
-            nc.gpsimd.tensor_scalar(out=mep[:], in0=mf[:], scalar1=LINK_EPS, scalar2=0.0, op0=ALU.mult, op1=ALU.add)
+            nc.vector.tensor_copy(out=b1f[:], in_=b1t[:])
+            nc.vector.tensor_copy(out=mf[:], in_=mbf[:])
+            nc.vector.tensor_tensor(out=msq[:], in0=mf[:], in1=mf[:], op=ALU.mult)
+            nc.vector.tensor_scalar(out=mep[:], in0=mf[:], scalar1=LINK_EPS, scalar2=None, op0=ALU.mult)
 
         def gate_bias():
             bf0 = pso.tile([P, CH], F32, name="bfp0", tag="ops")
@@ -208,12 +207,18 @@ def tile_embed_update_pa_kernel(tc, net_in, embeds, m, W1, b1, Wf, b_f, gamma, b
 
         def weights(G):
             k, n = first[G], GROUPS[G]
-            nc.gpsimd.tensor_tensor(out=wt[:, k:k + n], in0=sg[:, k:k + n], in1=msq[:, k:k + n], op=ALU.mult)
-            nc.gpsimd.tensor_tensor(out=st[:, 2, k:k + n], in0=wt[:, k:k + n], in1=mep[:, k:k + n], op=ALU.add)
+            for l in range(n):
+                nc.scalar.activation(out=st[:, 2, k + l:k + l + 1], in_=sg[:, k + l:k + l + 1], func=ACT.Identity,
+                                     bias=mep[:, k + l:k + l + 1], scale=msq[:, k + l:k + l + 1])
 
-        def pool_link(k):
+        def between():
+            nc.vector.tensor_tensor(out=st[:, 1, :], in0=st[:, 0, :], in1=gg[:], op=ALU.mult)
+
+        def pool_link(k, woven=None):
             op = banks["o%d" % k]
             for lo, hi in [(0, OUT)] if k < 12 else halves:
+                if k == LINKS - 1 and lo > 0:
+                    woven()
                 if k == 0:
                     nc.vector.tensor_scalar(out=acc[:, lo:hi], in0=op[:, lo:hi],
                                             scalar1=st[:, 2, k:k + 1], scalar2=None, op0=ALU.mult)
@@ -239,31 +244,20 @@ def tile_embed_update_pa_kernel(tc, net_in, embeds, m, W1, b1, Wf, b_f, gamma, b
                 quantise_w1(0)
                 regroup(nc.vector.tensor_copy, w1g[1][:], w1r[1][:])
             if i == 1 - LEAD_A:
-                small_prep()
                 regroup(nc.vector.tensor_copy, wfg[:], wfr[:])
+                small_prep()
             if has_c:
                 for l in range(GROUPS[gc]):
                     stage2(gc, l)
                 if not last:
                     for l in range(GROUPS[gc]):
                         gate(first[gc] + l)
-                    if gc == NG - 2:
-                        for k in range(first[gc], first[gc] + 2):
-                            nc.scalar.activation(out=st[:, 2, k:k + 1], in_=sg[:, k:k + 1], func=ACT.Identity,
-                                                 bias=mep[:, k:k + 1], scale=msq[:, k:k + 1])
-                    else:
-                        weights(gc)
+                    weights(gc)
                 if gc == NG - 2:
                     nc.scalar.activation(out=scr2[:, 0:OUT], in_=emb[:], func=ACT.Copy, scale=-1.0 / OUT,
                                          accum_out=nes[:, 0:1])
                     early_gates(NG - 1)
-                    for k in range(first[NG - 1], LINKS):
-                        nc.scalar.activation(out=st[:, 2, k:k + 1], in_=sg[:, k:k + 1], func=ACT.Identity,
-                                             bias=mep[:, k:k + 1], scale=msq[:, k:k + 1])
-                    nc.gpsimd.tensor_tensor(out=gg[:], in0=sg[:], in1=mf[:], op=ALU.mult)
-                    nc.gpsimd.tensor_scalar(out=st[:, 0, :], in0=gg[:], scalar1=LINK_EPS, scalar2=1.0,
-                                            op0=ALU.add, op1=ALU.mult)
-                    nc.gpsimd.tensor_tensor(out=st[:, 1, :], in0=st[:, 0, :], in1=gg[:], op=ALU.mult)
+                    weights(NG - 1)
                     bfp = psh.tile([P, CH], F32, name="bfp", tag="hp")
                     nc.tensor.matmul(out=bfp[:], lhsT=ones[:, 0:P], rhs=vecs[:, 0:CH], start=True, stop=True)
             if has_b:
@@ -273,19 +267,22 @@ def tile_embed_update_pa_kernel(tc, net_in, embeds, m, W1, b1, Wf, b_f, gamma, b
                     h_exit(gb, j)
                 if gb == 0:
                     gate_bias()
+            if last:
+                nc.vector.tensor_tensor(out=gg[:], in0=sg[:], in1=mf[:], op=ALU.mult)
             if has_c:
                 pool_link(first[gc])
+            if last:
+                nc.vector.tensor_scalar(out=st[:, 0, :], in0=gg[:], scalar1=LINK_EPS, scalar2=None, op0=ALU.add)
             if has_b:
                 share = TAIL_SHARE if gb >= NG - 2 else 0
                 w = GROUPS[gb] * TOK
                 if share:
                     regroup(nc.scalar.copy, hgr[gb][:, w - share:w, :], hpl[gb][:, :, w - share:w])
                 regroup(nc.vector.tensor_copy, hgr[gb][:, 0:w - share, :], hpl[gb][:, :, 0:w - share])
+            if has_c:
+                pool_link(first[gc] + 1, between)
             if last:
                 nc.vector.tensor_reduce(out=sums[:], in_=st[:], axis=AX.X, op=ALU.add)
-            if has_c:
-                pool_link(first[gc] + 1)
-            if last:
                 nc.vector.reciprocal(out=rl[:], in_=sums[:, 0:1])
                 nc.vector.tensor_scalar(out=sc[:], in0=sums[:, 1:2], scalar1=rl[:, 0:1], scalar2=rl[:, 0:1],
                                         op0=ALU.mult, op1=ALU.mult)
@@ -300,7 +297,7 @@ def tile_embed_update_pa_kernel(tc, net_in, embeds, m, W1, b1, Wf, b_f, gamma, b
                 for l in range(GROUPS[ga]):
                     transposes(first[ga] + l)
             if i == -LEAD_A or i == 1 - LEAD_A:
-                warm(3 if i == -LEAD_A else 1)
+                warm(5 if i == -LEAD_A else 2)
             if has_a:
                 for l in range(GROUPS[ga]):
                     x_exit(ga, l)

@@ -28,7 +28,7 @@ LEAD_A = 4
 LEAD_B = 2
 BANKS = {"x": 2, "h": 2, "o": 4}
 PINNED = True
-TAIL_SHARE = 128
+ON_VECTOR = (7,)
 GATE_COLS = 64
 
 FLOPS = 2 * TOK * LINKS * IN * HID + 2 * TOK * LINKS * HID * CH
@@ -126,7 +126,6 @@ def tile_embed_update_pa_kernel(tc, net_in, embeds, m, W1, b1, Wf, b_f, gamma, b
             nc.vector.quantize_mx(out=codes.bitcast(FP8X4), scales=scales, in_=grouped)
 
         def small_prep():
-            nc.vector.tensor_copy(out=b1f[:], in_=b1t[:])
             nc.vector.tensor_copy(out=mf[:], in_=mbf[:])
             nc.vector.tensor_tensor(out=msq[:], in0=mf[:], in1=mf[:], op=ALU.mult)
             nc.vector.tensor_scalar(out=mep[:], in0=mf[:], scalar1=LINK_EPS, scalar2=None, op0=ALU.mult)
@@ -157,7 +156,8 @@ def tile_embed_update_pa_kernel(tc, net_in, embeds, m, W1, b1, Wf, b_f, gamma, b
             n = GROUPS[G]
             dst = xg[G][:].bitcast(F32).rearrange("p (g l t u) -> p g l t u", g=2, l=n, t=TOK, u=2)
             xt = banks["x%d" % (first[G] + l)]
-            nc.scalar.copy(out=dst[:, :, l, :, :], in_=xt[:].rearrange("p (g u) t -> p g t u", g=2, u=2))
+            copy = nc.vector.tensor_copy if first[G] + l in ON_VECTOR else nc.scalar.copy
+            copy(out=dst[:, :, l, :, :], in_=xt[:].rearrange("p (g u) t -> p g t u", g=2, u=2))
 
         def stage1(G, b):
             n = GROUPS[G]
@@ -211,13 +211,23 @@ def tile_embed_update_pa_kernel(tc, net_in, embeds, m, W1, b1, Wf, b_f, gamma, b
                 nc.scalar.activation(out=st[:, 2, k + l:k + l + 1], in_=sg[:, k + l:k + l + 1], func=ACT.Identity,
                                      bias=mep[:, k + l:k + l + 1], scale=msq[:, k + l:k + l + 1])
 
+        def step_l():
+            nc.vector.tensor_scalar(out=st[:, 0, :], in0=gg[:], scalar1=LINK_EPS, scalar2=None, op0=ALU.add)
+
+        def step_q():
+            G = NG - 1
+            quantise(hc[G][:], hs[G][:], hgr[G][:].rearrange("p r j -> p (r j)"))
+
+        def step_sums():
+            nc.vector.tensor_reduce(out=sums[:], in_=st[:], axis=AX.X, op=ALU.add)
+
         def between():
             nc.vector.tensor_tensor(out=st[:, 1, :], in0=st[:, 0, :], in1=gg[:], op=ALU.mult)
 
         def pool_link(k, woven=None):
             op = banks["o%d" % k]
-            for lo, hi in [(0, OUT)] if k < 12 else halves:
-                if k == LINKS - 1 and lo > 0:
+            for lo, hi in [(0, OUT)] if k < 11 else halves:
+                if woven is not None and lo > 0:
                     woven()
                 if k == 0:
                     nc.vector.tensor_scalar(out=acc[:, lo:hi], in0=op[:, lo:hi],
@@ -244,6 +254,7 @@ def tile_embed_update_pa_kernel(tc, net_in, embeds, m, W1, b1, Wf, b_f, gamma, b
                 quantise_w1(0)
                 regroup(nc.vector.tensor_copy, w1g[1][:], w1r[1][:])
             if i == 1 - LEAD_A:
+                nc.vector.tensor_copy(out=b1f[:], in_=b1t[:])
                 regroup(nc.vector.tensor_copy, wfg[:], wfr[:])
                 small_prep()
             if has_c:
@@ -270,26 +281,21 @@ def tile_embed_update_pa_kernel(tc, net_in, embeds, m, W1, b1, Wf, b_f, gamma, b
             if last:
                 nc.vector.tensor_tensor(out=gg[:], in0=sg[:], in1=mf[:], op=ALU.mult)
             if has_c:
-                pool_link(first[gc])
+                pool_link(first[gc], step_l if last else None)
             if last:
-                nc.vector.tensor_scalar(out=st[:, 0, :], in0=gg[:], scalar1=LINK_EPS, scalar2=None, op0=ALU.add)
+                between()
             if has_b:
-                share = TAIL_SHARE if gb >= NG - 2 else 0
-                w = GROUPS[gb] * TOK
-                if share:
-                    regroup(nc.scalar.copy, hgr[gb][:, w - share:w, :], hpl[gb][:, :, w - share:w])
-                regroup(nc.vector.tensor_copy, hgr[gb][:, 0:w - share, :], hpl[gb][:, :, 0:w - share])
+                regroup(nc.vector.tensor_copy, hgr[gb][:], hpl[gb][:])
             if has_c:
-                pool_link(first[gc] + 1, between)
+                pool_link(first[gc] + 1, step_sums if last else step_q if gb == NG - 1 else None)
             if last:
-                nc.vector.tensor_reduce(out=sums[:], in_=st[:], axis=AX.X, op=ALU.add)
                 nc.vector.reciprocal(out=rl[:], in_=sums[:, 0:1])
                 nc.vector.tensor_scalar(out=sc[:], in0=sums[:, 1:2], scalar1=rl[:, 0:1], scalar2=rl[:, 0:1],
                                         op0=ALU.mult, op1=ALU.mult)
                 nc.vector.scalar_tensor_tensor(out=acc[:, 0:OUT], in0=bfp[:, 0:OUT], scalar=sums[:, 2:3],
                                                in1=acc[:, 0:OUT], op0=ALU.mult, op1=ALU.add, accum_out=sacc[:, 0:1])
                 nc.vector.tensor_scalar(out=nsc[:], in0=sc[:], scalar1=-1.0 / OUT, scalar2=None, op0=ALU.mult)
-            if has_b:
+            if has_b and not (has_c and gb == NG - 1):
                 quantise(hc[gb][:], hs[gb][:], hgr[gb][:].rearrange("p r j -> p (r j)"))
             if i == -LEAD_A:
                 warm(5)
@@ -297,7 +303,7 @@ def tile_embed_update_pa_kernel(tc, net_in, embeds, m, W1, b1, Wf, b_f, gamma, b
                 for l in range(GROUPS[ga]):
                     transposes(first[ga] + l)
             if i == -LEAD_A or i == 1 - LEAD_A:
-                warm(5 if i == -LEAD_A else 2)
+                warm(5 if i == -LEAD_A else 0)
             if has_a:
                 for l in range(GROUPS[ga]):
                     x_exit(ga, l)
@@ -316,7 +322,8 @@ def tile_embed_update_pa_kernel(tc, net_in, embeds, m, W1, b1, Wf, b_f, gamma, b
 
         ee = keep.tile([P, CH], F32, name="ee")
         negmu = keep.tile([P, 1], F32, name="negmu")
-        vs = keep.tile([P, 1], F32, name="vs")
+        vs = keep.tile([P, 2], F32, name="vs")
+        vt = keep.tile([P, 1], F32, name="vt")
         rstd = keep.tile([P, 1], F32, name="rstd")
         y1 = keep.tile([P, CH], F32, name="y1")
         yy = keep.tile([P, CH], F32, name="yy")
@@ -329,10 +336,13 @@ def tile_embed_update_pa_kernel(tc, net_in, embeds, m, W1, b1, Wf, b_f, gamma, b
         nc.vector.tensor_scalar(out=negmu[:], in0=sacc[:], scalar1=nsc[:, 0:1], scalar2=nes[:, 0:1],
                                 op0=ALU.mult, op1=ALU.add)
         residual(*halves[1])
-        nc.scalar.activation(out=scr2[:, 0:OUT], in_=ee[:, 0:OUT], func=ACT.Square,
-                             bias=negmu[:, 0:1], scale=1.0, accum_out=vs[:])
-        nc.scalar.activation(out=rstd[:], in_=vs[:], func=ACT.Abs_reciprocal_sqrt,
+        for h, (lo, hi) in enumerate(halves):
+            nc.scalar.activation(out=scr2[:, lo:hi], in_=ee[:, lo:hi], func=ACT.Square,
+                                 bias=negmu[:, 0:1], scale=1.0, accum_out=vs[:, h:h + 1])
+        nc.scalar.activation(out=vt[:], in_=vs[:, 0:1], func=ACT.Identity,
                              bias=epsln[:, 0:1], scale=1.0 / OUT)
+        nc.scalar.activation(out=rstd[:], in_=vs[:, 1:2], func=ACT.Abs_reciprocal_sqrt,
+                             bias=vt[:, 0:1], scale=1.0 / OUT)
         for lo, hi in halves:
             nc.vector.scalar_tensor_tensor(out=y1[:, lo:hi], in0=ee[:, lo:hi], scalar=negmu[:, 0:1],
                                            in1=gam[:, lo:hi], op0=ALU.add, op1=ALU.mult)

@@ -28,7 +28,6 @@ LEAD_A = 4
 LEAD_B = 2
 BANKS = {"x": 2, "h": 2, "o": 4}
 PINNED = True
-ON_VECTOR = (7,)
 GATE_COLS = 64
 
 FLOPS = 2 * TOK * LINKS * IN * HID + 2 * TOK * LINKS * HID * CH
@@ -83,10 +82,14 @@ def tile_embed_update_pa_kernel(tc, net_in, embeds, m, W1, b1, Wf, b_f, gamma, b
             nc.sync.dma_start(out=b1t[:], in_=b1.rearrange("(j p) -> p j", p=P))
         nc.sync.dma_start(out=wfr[:], in_=wfv)
         nc.sync.dma_start(out=vecs[0:1, 0:CH], in_=b_f.unsqueeze(0))
+        load_x(2)
         nc.sync.dma_start(out=mbf[:], in_=m2d)
+        load_x(3)
+        load_x(4)
+        load_x(5)
+        load_x(6)
+        load_x(7)
         nc.sync.dma_start(out=emb[:], in_=emb2d)
-        for c in range(2, LINKS // 2):
-            load_x(c)
         nc.sync.dma_start(out=vecs[0:1, CH:CH + OUT], in_=gamma.unsqueeze(0))
         nc.sync.dma_start(out=vecs[0:1, 2 * CH:2 * CH + OUT], in_=beta.unsqueeze(0))
 
@@ -156,8 +159,7 @@ def tile_embed_update_pa_kernel(tc, net_in, embeds, m, W1, b1, Wf, b_f, gamma, b
             n = GROUPS[G]
             dst = xg[G][:].bitcast(F32).rearrange("p (g l t u) -> p g l t u", g=2, l=n, t=TOK, u=2)
             xt = banks["x%d" % (first[G] + l)]
-            copy = nc.vector.tensor_copy if first[G] + l in ON_VECTOR else nc.scalar.copy
-            copy(out=dst[:, :, l, :, :], in_=xt[:].rearrange("p (g u) t -> p g t u", g=2, u=2))
+            nc.scalar.copy(out=dst[:, :, l, :, :], in_=xt[:].rearrange("p (g u) t -> p g t u", g=2, u=2))
 
         def stage1(G, b):
             n = GROUPS[G]
@@ -256,7 +258,6 @@ def tile_embed_update_pa_kernel(tc, net_in, embeds, m, W1, b1, Wf, b_f, gamma, b
             if i == 1 - LEAD_A:
                 nc.vector.tensor_copy(out=b1f[:], in_=b1t[:])
                 regroup(nc.vector.tensor_copy, wfg[:], wfr[:])
-                small_prep()
             if has_c:
                 for l in range(GROUPS[gc]):
                     stage2(gc, l)
@@ -302,8 +303,8 @@ def tile_embed_update_pa_kernel(tc, net_in, embeds, m, W1, b1, Wf, b_f, gamma, b
             if has_a:
                 for l in range(GROUPS[ga]):
                     transposes(first[ga] + l)
-            if i == -LEAD_A or i == 1 - LEAD_A:
-                warm(5 if i == -LEAD_A else 0)
+            if i == -LEAD_A:
+                warm(5)
             if has_a:
                 for l in range(GROUPS[ga]):
                     x_exit(ga, l)
@@ -312,6 +313,7 @@ def tile_embed_update_pa_kernel(tc, net_in, embeds, m, W1, b1, Wf, b_f, gamma, b
                 quantise_w1(1)
             if i == 1 - LEAD_A:
                 quantise(wfc[:], wfs[:], wfg[:].rearrange("p c t -> p (c t)"))
+                small_prep()
 
         nc.scalar.activation(out=scr[:], in_=sg[:, LINKS - 1:LINKS], func=ACT.Abs_reciprocal_sqrt,
                              bias=epsln[:, 0:1], scale=1.0)

@@ -28,6 +28,7 @@ LEAD_A = 4
 LEAD_B = 2
 BANKS = {"x": 2, "h": 2, "o": 4}
 PINNED = True
+SHARE = 128
 GATE_COLS = 64
 
 FLOPS = 2 * TOK * LINKS * IN * HID + 2 * TOK * LINKS * HID * CH
@@ -115,10 +116,15 @@ def tile_embed_update_pa_kernel(tc, net_in, embeds, m, W1, b1, Wf, b_f, gamma, b
             hc.append(keep.tile([P, n * TOK], U32, name="hc%d" % G, align_bytes=64))
             hs.append(keep.tile([P, n * TOK], U8, name="hs%d" % G, align_bytes=64))
         sg = keep.tile([P, LINKS], F32, name="sg")
-        st = keep.tile([P, 3, LINKS], F32, name="st")
+        st = keep.tile([P, LINKS], F32, name="st")
         acc = keep.tile([P, CH], F32, name="acc")
         gg = keep.tile([P, LINKS], F32, name="gg")
-        sums = keep.tile([P, 3], F32, name="sums")
+        gsum = keep.tile([P, 1], F32, name="gsum")
+        lsum = keep.tile([P, 1], F32, name="lsum")
+        lgsum = keep.tile([P, 1], F32, name="lgsum")
+        wsum = keep.tile([P, 1], F32, name="wsum")
+        lg = keep.tile([P, LINKS], F32, name="lg")
+        wcopy = keep.tile([P, LINKS], F32, name="wcopy")
         banks = {}
 
         def regroup(copy, dst, src):
@@ -195,36 +201,44 @@ def tile_embed_update_pa_kernel(tc, net_in, embeds, m, W1, b1, Wf, b_f, gamma, b
             nc.scalar.activation(out=sg[:, k:k + 1], in_=banks["o%d" % k][:, OUT:CH], func=ACT.Sigmoid,
                                  bias=bgate[:, 0:1], scale=1.0)
 
-        def early_gates(G):
-            k, n = first[G], GROUPS[G]
-            gl = psx.tile([P, n, GATE_COLS], F32, name="gl", tag="xt")
-            for l in range(n):
-                nc.tensor.matmul_mx(out=gl[:, l, :],
-                                    lhsT=hc[G][:, l * TOK:(l + 1) * TOK].bitcast(FP8X4),
-                                    lhsT_scale=hs[G][:, l * TOK:(l + 1) * TOK],
-                                    rhs=wfc[:, CH - GATE_COLS:CH].bitcast(FP8X4),
-                                    rhs_scale=wfs[:, CH - GATE_COLS:CH], start=True, stop=True)
-            nc.scalar.activation(out=sg[:, k:k + n], in_=gl[:, :, GATE_COLS - 1], func=ACT.Sigmoid,
+        def early_gate(l):
+            G = NG - 1
+            k = first[G] + l
+            gl = psx.tile([P, GATE_COLS], F32, name="gl", tag="xt")
+            nc.tensor.matmul_mx(out=gl[:],
+                                lhsT=hc[G][:, l * TOK:(l + 1) * TOK].bitcast(FP8X4),
+                                lhsT_scale=hs[G][:, l * TOK:(l + 1) * TOK],
+                                rhs=wfc[:, CH - GATE_COLS:CH].bitcast(FP8X4),
+                                rhs_scale=wfs[:, CH - GATE_COLS:CH], start=True, stop=True)
+            nc.scalar.activation(out=sg[:, k:k + 1], in_=gl[:, GATE_COLS - 1:GATE_COLS], func=ACT.Sigmoid,
                                  bias=bgate[:, 0:1], scale=1.0)
+            weight(k)
 
-        def weights(G):
-            k, n = first[G], GROUPS[G]
-            for l in range(n):
-                nc.scalar.activation(out=st[:, 2, k + l:k + l + 1], in_=sg[:, k + l:k + l + 1], func=ACT.Identity,
-                                     bias=mep[:, k + l:k + l + 1], scale=msq[:, k + l:k + l + 1])
+        def weight(k):
+            nc.scalar.activation(out=st[:, k:k + 1], in_=sg[:, k:k + 1], func=ACT.Identity,
+                                 bias=mep[:, k:k + 1], scale=msq[:, k:k + 1])
 
         def step_l():
-            nc.vector.tensor_scalar(out=st[:, 0, :], in0=gg[:], scalar1=LINK_EPS, scalar2=None, op0=ALU.add)
+            nc.vector.tensor_scalar(out=lsum[:], in0=gsum[:], scalar1=LINKS * LINK_EPS, scalar2=None, op0=ALU.add)
+            nc.vector.scalar_tensor_tensor(out=lg[:], in0=gg[:], scalar=LINK_EPS, in1=gg[:],
+                                           op0=ALU.add, op1=ALU.mult, accum_out=lgsum[:])
+
+        def regroup_last(copy, l):
+            G = NG - 1
+            cols = slice(l * TOK, (l + 1) * TOK)
+            regroup(copy, hgr[G][:, cols, :], hpl[G][:, :, cols])
+
+        def quantise_last(l):
+            G = NG - 1
+            cols = slice(l * TOK, (l + 1) * TOK)
+            quantise(hc[G][:, cols], hs[G][:, cols], hgr[G][:, cols, :].rearrange("p r j -> p (r j)"))
 
         def step_q():
-            G = NG - 1
-            quantise(hc[G][:], hs[G][:], hgr[G][:].rearrange("p r j -> p (r j)"))
+            quantise_last(0)
 
-        def step_sums():
-            nc.vector.tensor_reduce(out=sums[:], in_=st[:], axis=AX.X, op=ALU.add)
-
-        def between():
-            nc.vector.tensor_tensor(out=st[:, 1, :], in0=st[:, 0, :], in1=gg[:], op=ALU.mult)
+        def step_sc():
+            nc.vector.tensor_scalar(out=sc[:], in0=lgsum[:], scalar1=rl[:, 0:1], scalar2=rl[:, 0:1],
+                                    op0=ALU.mult, op1=ALU.mult)
 
         def pool_link(k, woven=None):
             op = banks["o%d" % k]
@@ -233,14 +247,15 @@ def tile_embed_update_pa_kernel(tc, net_in, embeds, m, W1, b1, Wf, b_f, gamma, b
                     woven()
                 if k == 0:
                     nc.vector.tensor_scalar(out=acc[:, lo:hi], in0=op[:, lo:hi],
-                                            scalar1=st[:, 2, k:k + 1], scalar2=None, op0=ALU.mult)
+                                            scalar1=st[:, k:k + 1], scalar2=None, op0=ALU.mult)
                 else:
                     nc.vector.scalar_tensor_tensor(out=acc[:, lo:hi], in0=op[:, lo:hi],
-                                                   scalar=st[:, 2, k:k + 1], in1=acc[:, lo:hi],
+                                                   scalar=st[:, k:k + 1], in1=acc[:, lo:hi],
                                                    op0=ALU.mult, op1=ALU.add)
 
         halves = [(0, 256), (256, OUT)]
-        sacc = keep.tile([P, 1], F32, name="sacc")
+        sacc = keep.tile([P, 2], F32, name="sacc")
+        nmu0 = keep.tile([P, 1], F32, name="nmu0")
         nes = keep.tile([P, 1], F32, name="nes")
         scr2 = keep.tile([P, CH], F32, name="scr2")
         rl = keep.tile([P, 1], F32, name="rl")
@@ -254,22 +269,25 @@ def tile_embed_update_pa_kernel(tc, net_in, embeds, m, W1, b1, Wf, b_f, gamma, b
             if i == -LEAD_A:
                 regroup(nc.vector.tensor_copy, w1g[0][:], w1r[0][:])
                 quantise_w1(0)
-                regroup(nc.vector.tensor_copy, w1g[1][:], w1r[1][:])
+                regroup(nc.vector.tensor_copy, w1g[1][:, 0:HID - SHARE, :], w1r[1][:, :, 0:HID - SHARE])
             if i == 1 - LEAD_A:
                 nc.vector.tensor_copy(out=b1f[:], in_=b1t[:])
-                regroup(nc.vector.tensor_copy, wfg[:], wfr[:])
-            if has_c:
+                regroup(nc.vector.tensor_copy, wfg[:, 0:CH // 2, :], wfr[:, :, 0:CH // 2])
+            if has_c and not last:
                 for l in range(GROUPS[gc]):
                     stage2(gc, l)
                 if not last:
                     for l in range(GROUPS[gc]):
                         gate(first[gc] + l)
-                    weights(gc)
+                    for l in range(GROUPS[gc]):
+                        weight(first[gc] + l)
                 if gc == NG - 2:
                     nc.scalar.activation(out=scr2[:, 0:OUT], in_=emb[:], func=ACT.Copy, scale=-1.0 / OUT,
                                          accum_out=nes[:, 0:1])
-                    early_gates(NG - 1)
-                    weights(NG - 1)
+                    for l in range(2):
+                        early_gate(l)
+                        stage2(NG - 1, l)
+                    nc.scalar.activation(out=wcopy[:], in_=st[:], func=ACT.Copy, accum_out=wsum[:])
                     bfp = psh.tile([P, CH], F32, name="bfp", tag="hp")
                     nc.tensor.matmul(out=bfp[:], lhsT=ones[:, 0:P], rhs=vecs[:, 0:CH], start=True, stop=True)
             if has_b:
@@ -280,23 +298,32 @@ def tile_embed_update_pa_kernel(tc, net_in, embeds, m, W1, b1, Wf, b_f, gamma, b
                 if gb == 0:
                     gate_bias()
             if last:
-                nc.vector.tensor_tensor(out=gg[:], in0=sg[:], in1=mf[:], op=ALU.mult)
+                nc.vector.scalar_tensor_tensor(out=gg[:], in0=sg[:], scalar=1.0, in1=mf[:],
+                                               op0=ALU.mult, op1=ALU.mult, accum_out=gsum[:])
             if has_c:
                 pool_link(first[gc], step_l if last else None)
             if last:
-                between()
-            if has_b:
+                nc.vector.reciprocal(out=rl[:], in_=lsum[:])
+            if has_c and gb == NG - 1:
+                regroup_last(nc.vector.tensor_copy, 0)
+                regroup_last(nc.scalar.copy, 1)
+            elif has_b:
                 regroup(nc.vector.tensor_copy, hgr[gb][:], hpl[gb][:])
             if has_c:
-                pool_link(first[gc] + 1, step_sums if last else step_q if gb == NG - 1 else None)
+                pool_link(first[gc] + 1, step_sc if last else step_q if gb == NG - 1 else None)
             if last:
-                nc.vector.reciprocal(out=rl[:], in_=sums[:, 0:1])
-                nc.vector.tensor_scalar(out=sc[:], in0=sums[:, 1:2], scalar1=rl[:, 0:1], scalar2=rl[:, 0:1],
-                                        op0=ALU.mult, op1=ALU.mult)
-                nc.vector.scalar_tensor_tensor(out=acc[:, 0:OUT], in0=bfp[:, 0:OUT], scalar=sums[:, 2:3],
-                                               in1=acc[:, 0:OUT], op0=ALU.mult, op1=ALU.add, accum_out=sacc[:, 0:1])
                 nc.vector.tensor_scalar(out=nsc[:], in0=sc[:], scalar1=-1.0 / OUT, scalar2=None, op0=ALU.mult)
-            if has_b and not (has_c and gb == NG - 1):
+                for h, (lo, hi) in enumerate(halves):
+                    nc.vector.scalar_tensor_tensor(out=acc[:, lo:hi], in0=bfp[:, lo:hi], scalar=wsum[:, 0:1],
+                                                   in1=acc[:, lo:hi], op0=ALU.mult, op1=ALU.add,
+                                                   accum_out=sacc[:, h:h + 1])
+                nc.vector.tensor_scalar(out=nmu0[:], in0=sacc[:, 0:1], scalar1=nsc[:, 0:1], scalar2=nes[:, 0:1],
+                                        op0=ALU.mult, op1=ALU.add)
+            if gb == 0:
+                quantise(wfc[:], wfs[:], wfg[:].rearrange("p c t -> p (c t)"))
+            if has_c and gb == NG - 1:
+                quantise_last(1)
+            elif has_b:
                 quantise(hc[gb][:], hs[gb][:], hgr[gb][:].rearrange("p r j -> p (r j)"))
             if i == -LEAD_A:
                 warm(5)
@@ -308,12 +335,15 @@ def tile_embed_update_pa_kernel(tc, net_in, embeds, m, W1, b1, Wf, b_f, gamma, b
             if has_a:
                 for l in range(GROUPS[ga]):
                     x_exit(ga, l)
+                if ga == 0:
+                    regroup(nc.scalar.copy, w1g[1][:, HID - SHARE:HID, :], w1r[1][:, :, HID - SHARE:HID])
                 quantise(xc[ga][:], xs[ga][:], xg[ga][:])
+            if gb == 0:
+                small_prep()
             if i == -LEAD_A:
                 quantise_w1(1)
             if i == 1 - LEAD_A:
-                quantise(wfc[:], wfs[:], wfg[:].rearrange("p c t -> p (c t)"))
-                small_prep()
+                regroup(nc.vector.tensor_copy, wfg[:, CH // 2:CH, :], wfr[:, :, CH // 2:CH])
 
         nc.scalar.activation(out=scr[:], in_=sg[:, LINKS - 1:LINKS], func=ACT.Abs_reciprocal_sqrt,
                              bias=epsln[:, 0:1], scale=1.0)
@@ -335,7 +365,7 @@ def tile_embed_update_pa_kernel(tc, net_in, embeds, m, W1, b1, Wf, b_f, gamma, b
                                            in1=emb[:, lo:hi], op0=ALU.mult, op1=ALU.add)
 
         residual(*halves[0])
-        nc.vector.tensor_scalar(out=negmu[:], in0=sacc[:], scalar1=nsc[:, 0:1], scalar2=nes[:, 0:1],
+        nc.vector.tensor_scalar(out=negmu[:], in0=sacc[:, 1:2], scalar1=nsc[:, 0:1], scalar2=nmu0[:, 0:1],
                                 op0=ALU.mult, op1=ALU.add)
         residual(*halves[1])
         for h, (lo, hi) in enumerate(halves):

@@ -99,22 +99,22 @@ def tile_embed_update_pa_kernel(tc, net_in, embeds, m, W1, b1, Wf, b_f, gamma, b
         msq = keep.tile([P, LINKS], F32, name="msq")
         mep = keep.tile([P, LINKS], F32, name="mep")
         bgate = keep.tile([P, 1], F32, name="bgate")
-        w1c = keep.tile([P, 2 * HID], U32, name="w1c", align_bytes=64)
-        w1s = keep.tile([P, 2 * HID], U8, name="w1s", align_bytes=64)
+        w1c = keep.tile([P, 2 * HID], U32, name="w1c", align_bytes=256)
+        w1s = keep.tile([P, 2 * HID], U8, name="w1s", align_bytes=256)
         w1g = [keep.tile([P, HID, 4], BF16, name="w1g%d" % g, align_bytes=64) for g in range(2)]
-        wfc = keep.tile([P, CH], U32, name="wfc", align_bytes=64)
-        wfs = keep.tile([P, CH], U8, name="wfs", align_bytes=64)
+        wfc = keep.tile([P, CH], U32, name="wfc", align_bytes=256)
+        wfs = keep.tile([P, CH], U8, name="wfs", align_bytes=256)
         wfg = keep.tile([P, CH, 4], BF16, name="wfg", align_bytes=64)
         first = [sum(GROUPS[:i]) for i in range(len(GROUPS))]
         xg, xc, xs, hpl, hgr, hc, hs = [], [], [], [], [], [], []
         for G, n in enumerate(GROUPS):
             xg.append(keep.tile([P, 2 * n * TOK * 4], BF16, name="xg%d" % G, align_bytes=64))
-            xc.append(keep.tile([P, 2 * n * TOK], U32, name="xc%d" % G, align_bytes=64))
-            xs.append(keep.tile([P, 2 * n * TOK], U8, name="xs%d" % G, align_bytes=64))
+            xc.append(keep.tile([P, 2 * n * TOK], U32, name="xc%d" % G, align_bytes=256))
+            xs.append(keep.tile([P, 2 * n * TOK], U8, name="xs%d" % G, align_bytes=256))
             hpl.append(keep.tile([P, 4, n * TOK], BF16, name="hpl%d" % G))
             hgr.append(keep.tile([P, n * TOK, 4], BF16, name="hgr%d" % G, align_bytes=64))
-            hc.append(keep.tile([P, n * TOK], U32, name="hc%d" % G, align_bytes=64))
-            hs.append(keep.tile([P, n * TOK], U8, name="hs%d" % G, align_bytes=64))
+            hc.append(keep.tile([P, n * TOK], U32, name="hc%d" % G, align_bytes=256))
+            hs.append(keep.tile([P, n * TOK], U8, name="hs%d" % G, align_bytes=256))
         sg = keep.tile([P, LINKS], F32, name="sg")
         st = keep.tile([P, LINKS], F32, name="st")
         acc = keep.tile([P, CH], F32, name="acc")
@@ -282,12 +282,12 @@ def tile_embed_update_pa_kernel(tc, net_in, embeds, m, W1, b1, Wf, b_f, gamma, b
                     for l in range(GROUPS[gc]):
                         weight(first[gc] + l)
                 if gc == NG - 2:
-                    nc.scalar.activation(out=scr2[:, 0:OUT], in_=emb[:], func=ACT.Copy, scale=-1.0 / OUT,
-                                         accum_out=nes[:, 0:1])
                     for l in range(2):
                         early_gate(l)
                         stage2(NG - 1, l)
                     nc.scalar.activation(out=wcopy[:], in_=st[:], func=ACT.Copy, accum_out=wsum[:])
+                    nc.scalar.activation(out=scr2[:, 0:OUT], in_=emb[:], func=ACT.Copy, scale=-1.0 / OUT,
+                                         accum_out=nes[:, 0:1])
                     bfp = psh.tile([P, CH], F32, name="bfp", tag="hp")
                     nc.tensor.matmul(out=bfp[:], lhsT=ones[:, 0:P], rhs=vecs[:, 0:CH], start=True, stop=True)
             if has_b:

@@ -53,7 +53,7 @@ def tile_embed_update_pa_kernel(tc, net_in, embeds, m, W1, b1, Wf, b_f, gamma, b
 
         ident = keep.tile([P, P], F32, name="ident")
         masks.make_identity(nc, ident[:])
-        vecs = keep.tile([P, 3 * CH], BF16, name="vecs")
+        vecs = keep.tile([P, 4 * CH], BF16, name="vecs")
         nc.vector.memset(vecs[:].bitcast(I32), 0)
         ones = keep.tile([P, CH], BF16, name="ones")
         nc.vector.memset(ones[:], 1.0)
@@ -66,7 +66,6 @@ def tile_embed_update_pa_kernel(tc, net_in, embeds, m, W1, b1, Wf, b_f, gamma, b
         w1r = [keep.tile([P, 4, HID], BF16, name="w1r%d" % g) for g in range(2)]
         wfr = keep.tile([P, 4, CH], BF16, name="wfr")
         xr = [keep.tile([P, 2 * IN], BF16, name="xr%d" % c) for c in range(LINKS // 2)]
-        b1t = keep.tile([P, 4], BF16, name="b1t")
         emb = keep.tile([P, OUT], BF16, name="emb")
 
         def load_w1(g):
@@ -78,9 +77,8 @@ def tile_embed_update_pa_kernel(tc, net_in, embeds, m, W1, b1, Wf, b_f, gamma, b
         load_w1(0)
         load_x(0)
         load_w1(1)
+        nc.sync.dma_start(out=vecs[0:1, 3 * CH:4 * CH], in_=b1.unsqueeze(0))
         load_x(1)
-        with nc.allow_non_contiguous_dma(reason="512 bias values, one to a partition and chunk"):
-            nc.sync.dma_start(out=b1t[:], in_=b1.rearrange("(j p) -> p j", p=P))
         nc.sync.dma_start(out=wfr[:], in_=wfv)
         nc.sync.dma_start(out=vecs[0:1, 0:CH], in_=b_f.unsqueeze(0))
         load_x(2)
@@ -94,7 +92,7 @@ def tile_embed_update_pa_kernel(tc, net_in, embeds, m, W1, b1, Wf, b_f, gamma, b
         nc.sync.dma_start(out=vecs[0:1, CH:CH + OUT], in_=gamma.unsqueeze(0))
         nc.sync.dma_start(out=vecs[0:1, 2 * CH:2 * CH + OUT], in_=beta.unsqueeze(0))
 
-        b1f = keep.tile([P, 4], F32, name="b1f")
+        b1f = keep.tile([P, 8], F32, name="b1f")
         mf = keep.tile([P, LINKS], F32, name="mf")
         msq = keep.tile([P, LINKS], F32, name="msq")
         mep = keep.tile([P, LINKS], F32, name="mep")
@@ -153,6 +151,13 @@ def tile_embed_update_pa_kernel(tc, net_in, embeds, m, W1, b1, Wf, b_f, gamma, b
             for r in range(count):
                 nc.tensor.matmul(out=wb[:], lhsT=ones[:, 0:P], rhs=ones[:], start=True, stop=True)
 
+        def spread_b1():
+            bp = pso.tile([P, CH], F32, name="b1p", tag="ops")
+            banks["b1"] = bp
+            for j in range(4):
+                lo = 3 * CH + j * P
+                nc.tensor.matmul(out=bp[:, 2 * j:2 * j + 2], lhsT=vecs[:, lo:lo + P], rhs=ones[:, 0:2], start=True, stop=True)
+
         def transposes(k):
             words = xr[k // 2][:].bitcast(F32)
             xt = psx.tile([P, 4, TOK], F32, name="xt", tag="xt")
@@ -187,7 +192,7 @@ def tile_embed_update_pa_kernel(tc, net_in, embeds, m, W1, b1, Wf, b_f, gamma, b
             per = 4 // GROUPS[G]
             hp = banks["h%d_%d" % (G, j // per)]
             nc.scalar.activation(out=hpl[G][:, j, :], in_=hp[:, j % per, :], func=ACT.Relu,
-                                 bias=b1f[:, j:j + 1], scale=1.0)
+                                 bias=b1f[:, 2 * j:2 * j + 1], scale=1.0)
 
         def stage2(G, l):
             op = pso.tile([P, CH], F32, name="op", tag="ops")
@@ -271,7 +276,7 @@ def tile_embed_update_pa_kernel(tc, net_in, embeds, m, W1, b1, Wf, b_f, gamma, b
                 quantise_w1(0)
                 regroup(nc.vector.tensor_copy, w1g[1][:, 0:HID - SHARE, :], w1r[1][:, :, 0:HID - SHARE])
             if i == 1 - LEAD_A:
-                nc.vector.tensor_copy(out=b1f[:], in_=b1t[:])
+                nc.vector.tensor_copy(out=b1f[:], in_=banks["b1"][:, 0:8])
                 regroup(nc.vector.tensor_copy, wfg[:, 0:CH // 2, :], wfr[:, :, 0:CH // 2])
             if has_c and not last:
                 for l in range(GROUPS[gc]):
@@ -331,7 +336,8 @@ def tile_embed_update_pa_kernel(tc, net_in, embeds, m, W1, b1, Wf, b_f, gamma, b
                 for l in range(GROUPS[ga]):
                     transposes(first[ga] + l)
             if i == -LEAD_A:
-                warm(5)
+                warm(3)
+                spread_b1()
             if has_a:
                 for l in range(GROUPS[ga]):
                     x_exit(ga, l)

@@ -126,8 +126,8 @@ def tile_embed_update_pa_kernel(tc, net_in, embeds, m, W1, b1, Wf, b_f, gamma, b
         banks = {}
 
         def regroup(copy, dst, src):
-            copy(out=dst.rearrange("p (c i) t -> p c t i", i=4),
-                 in_=src.rearrange("p t (c i) -> p c t i", i=4))
+            copy(out=dst.rearrange("p (c i) t -> p c t i", i=8),
+                 in_=src.rearrange("p t (c i) -> p c t i", i=8))
 
         def quantise(codes, scales, grouped):
             nc.vector.quantize_mx(out=codes.bitcast(FP8X4), scales=scales, in_=grouped)

@@ -41,7 +41,7 @@ def tile_embed_update_pa_kernel(tc, net_in, embeds, m, W1, b1, Wf, b_f, gamma, b
     emb2d = embeds.rearrange("b s c -> (b s) c")
     out2d = out.rearrange("b s c -> (b s) c")
     w1v = W1.rearrange("(g u p e) c -> g p u (e c)", g=2, u=2, p=P, e=2)
-    wfv = Wf.rearrange("(t p) c -> p t c", t=4, p=P)
+    wfv = Wf.rearrange("(p t) c -> p t c", t=4, p=P)
 
     with ExitStack() as ctx:
         keep = ctx.enter_context(tc.tile_pool(name="keep", bufs=1))
@@ -78,9 +78,9 @@ def tile_embed_update_pa_kernel(tc, net_in, embeds, m, W1, b1, Wf, b_f, gamma, b
         load_x(0)
         load_w1(1)
         nc.sync.dma_start(out=vecs[0:1, 3 * CH:4 * CH], in_=b1.unsqueeze(0))
+        nc.sync.dma_start(out=vecs[0:1, 0:CH], in_=b_f.unsqueeze(0))
         load_x(1)
         nc.sync.dma_start(out=wfr[:], in_=wfv)
-        nc.sync.dma_start(out=vecs[0:1, 0:CH], in_=b_f.unsqueeze(0))
         load_x(2)
         nc.sync.dma_start(out=mbf[:], in_=m2d)
         load_x(3)
@@ -92,11 +92,10 @@ def tile_embed_update_pa_kernel(tc, net_in, embeds, m, W1, b1, Wf, b_f, gamma, b
         nc.sync.dma_start(out=vecs[0:1, CH:CH + OUT], in_=gamma.unsqueeze(0))
         nc.sync.dma_start(out=vecs[0:1, 2 * CH:2 * CH + OUT], in_=beta.unsqueeze(0))
 
-        b1f = keep.tile([P, 8], F32, name="b1f")
+        b1f = keep.tile([P, 10], F32, name="b1f")
         mf = keep.tile([P, LINKS], F32, name="mf")
         msq = keep.tile([P, LINKS], F32, name="msq")
         mep = keep.tile([P, LINKS], F32, name="mep")
-        bgate = keep.tile([P, 1], F32, name="bgate")
         w1c = keep.tile([P, 2 * HID], U32, name="w1c", align_bytes=256)
         w1s = keep.tile([P, 2 * HID], U8, name="w1s", align_bytes=256)
         w1g = [keep.tile([P, HID, 4], BF16, name="w1g%d" % g, align_bytes=64) for g in range(2)]
@@ -129,18 +128,17 @@ def tile_embed_update_pa_kernel(tc, net_in, embeds, m, W1, b1, Wf, b_f, gamma, b
             copy(out=dst.rearrange("p (c i) t -> p c t i", i=8),
                  in_=src.rearrange("p t (c i) -> p c t i", i=8))
 
+        def regroup_w1(copy, g, lo, hi):
+            copy(out=w1g[g][:].rearrange("p (i c) t -> p c t i", i=4)[:, lo:hi, :, :],
+                 in_=w1r[g][:].rearrange("p t (c i) -> p c t i", i=4)[:, lo:hi, :, :])
+
         def quantise(codes, scales, grouped):
             nc.vector.quantize_mx(out=codes.bitcast(FP8X4), scales=scales, in_=grouped)
 
         def small_prep():
             nc.vector.tensor_copy(out=mf[:], in_=mbf[:])
-            nc.vector.tensor_tensor(out=msq[:], in0=mf[:], in1=mf[:], op=ALU.mult)
-            nc.vector.tensor_scalar(out=mep[:], in0=mf[:], scalar1=LINK_EPS, scalar2=None, op0=ALU.mult)
-
-        def gate_bias():
-            bf0 = pso.tile([P, CH], F32, name="bfp0", tag="ops")
-            nc.tensor.matmul(out=bf0[:], lhsT=ones[:, 0:P], rhs=vecs[:, 0:CH], start=True, stop=True)
-            nc.vector.tensor_copy(out=bgate[:], in_=bf0[:, OUT:CH])
+            nc.vector.tensor_tensor(out=msq[:], in0=mbf[:], in1=mbf[:], op=ALU.mult)
+            nc.vector.tensor_scalar(out=mep[:], in0=mbf[:], scalar1=LINK_EPS, scalar2=None, op0=ALU.mult)
 
         def quantise_w1(g):
             quantise(w1c[:, g * HID:(g + 1) * HID], w1s[:, g * HID:(g + 1) * HID],
@@ -155,8 +153,8 @@ def tile_embed_update_pa_kernel(tc, net_in, embeds, m, W1, b1, Wf, b_f, gamma, b
             bp = pso.tile([P, CH], F32, name="b1p", tag="ops")
             banks["b1"] = bp
             for j in range(4):
-                lo = 3 * CH + j * P
-                nc.tensor.matmul(out=bp[:, 2 * j:2 * j + 2], lhsT=vecs[:, lo:lo + P], rhs=ones[:, 0:2], start=True, stop=True)
+                nc.tensor.matmul(out=bp[:, 2 * j:2 * j + 2], lhsT=vecs[:, 3 * CH + j:4 * CH:4], rhs=ones[:, 0:2], start=True, stop=True)
+            nc.tensor.matmul(out=bp[:, 8:10], lhsT=ones[:, 0:P], rhs=vecs[:, CH - 2:CH], start=True, stop=True)
 
         def transposes(k):
             words = xr[k // 2][:].bitcast(F32)
@@ -204,7 +202,7 @@ def tile_embed_update_pa_kernel(tc, net_in, embeds, m, W1, b1, Wf, b_f, gamma, b
 
         def gate(k):
             nc.scalar.activation(out=sg[:, k:k + 1], in_=banks["o%d" % k][:, OUT:CH], func=ACT.Sigmoid,
-                                 bias=bgate[:, 0:1], scale=1.0)
+                                 bias=b1f[:, 9:10], scale=1.0)
 
         def early_gate(l):
             G = NG - 1
@@ -216,7 +214,7 @@ def tile_embed_update_pa_kernel(tc, net_in, embeds, m, W1, b1, Wf, b_f, gamma, b
                                 rhs=wfc[:, CH - GATE_COLS:CH].bitcast(FP8X4),
                                 rhs_scale=wfs[:, CH - GATE_COLS:CH], start=True, stop=True)
             nc.scalar.activation(out=sg[:, k:k + 1], in_=gl[:, GATE_COLS - 1:GATE_COLS], func=ACT.Sigmoid,
-                                 bias=bgate[:, 0:1], scale=1.0)
+                                 bias=b1f[:, 9:10], scale=1.0)
             weight(k)
 
         def weight(k):
@@ -272,11 +270,11 @@ def tile_embed_update_pa_kernel(tc, net_in, embeds, m, W1, b1, Wf, b_f, gamma, b
             has_a, has_b, has_c = ga < NG, 0 <= gb < NG, gc >= 0
             last = i == NG - 1
             if i == -LEAD_A:
-                regroup(nc.vector.tensor_copy, w1g[0][:], w1r[0][:])
+                regroup_w1(nc.vector.tensor_copy, 0, 0, P)
                 quantise_w1(0)
-                regroup(nc.vector.tensor_copy, w1g[1][:, 0:HID - SHARE, :], w1r[1][:, :, 0:HID - SHARE])
+                regroup_w1(nc.vector.tensor_copy, 1, 0, P - SHARE // 4)
             if i == 1 - LEAD_A:
-                nc.vector.tensor_copy(out=b1f[:], in_=banks["b1"][:, 0:8])
+                nc.vector.tensor_copy(out=b1f[:], in_=banks["b1"][:, 0:10])
                 regroup(nc.vector.tensor_copy, wfg[:, 0:CH // 2, :], wfr[:, :, 0:CH // 2])
             if has_c and not last:
                 for l in range(GROUPS[gc]):
@@ -300,8 +298,6 @@ def tile_embed_update_pa_kernel(tc, net_in, embeds, m, W1, b1, Wf, b_f, gamma, b
                     stage1(gb, b)
                 for j in range(4):
                     h_exit(gb, j)
-                if gb == 0:
-                    gate_bias()
             if last:
                 nc.vector.scalar_tensor_tensor(out=gg[:], in0=sg[:], scalar=1.0, in1=mf[:],
                                                op0=ALU.mult, op1=ALU.mult, accum_out=gsum[:])
@@ -342,7 +338,7 @@ def tile_embed_update_pa_kernel(tc, net_in, embeds, m, W1, b1, Wf, b_f, gamma, b
                 for l in range(GROUPS[ga]):
                     x_exit(ga, l)
                 if ga == 0:
-                    regroup(nc.scalar.copy, w1g[1][:, HID - SHARE:HID, :], w1r[1][:, :, HID - SHARE:HID])
+                    regroup_w1(nc.scalar.copy, 1, P - SHARE // 4, P)
                 quantise(xc[ga][:], xs[ga][:], xg[ga][:])
             if gb == 0:
                 small_prep()

@@ -57,11 +57,13 @@ def tile_embed_update_pa_kernel(tc, net_in, embeds, m, W1, b1, Wf, b_f, gamma, b
         nc.vector.memset(vecs[:].bitcast(I32), 0)
         ones = keep.tile([P, CH], BF16, name="ones")
         nc.vector.memset(ones[:], 1.0)
+        trig = keep.tile([P, CH], BF16, name="trig")
+        nc.vector.memset(trig[:], 1.0)
         epsln = keep.tile([P, 1], F32, name="epsln")
         nc.vector.memset(epsln[:], LN_EPS)
 
         scr = keep.tile([P, 1], F32, name="scr")
-        nc.scalar.activation(out=scr[:], in_=epsln[:], func=ACT.Sigmoid)
+        nc.scalar.activation(out=trig[:, 0:1], in_=epsln[:], func=ACT.Sigmoid)
         mbf = keep.tile([P, LINKS], BF16, name="mbf")
         w1r = [keep.tile([P, 4, HID], BF16, name="w1r%d" % g) for g in range(2)]
         wfr = keep.tile([P, 4, CH], BF16, name="wfr")
@@ -144,10 +146,10 @@ def tile_embed_update_pa_kernel(tc, net_in, embeds, m, W1, b1, Wf, b_f, gamma, b
             quantise(w1c[:, g * HID:(g + 1) * HID], w1s[:, g * HID:(g + 1) * HID],
                      w1g[g][:].rearrange("p c t -> p (c t)"))
 
-        def warm(count):
+        def warm(*operands):
             wb = pso.tile([P, CH], F32, name="warmup", tag="ops")
-            for r in range(count):
-                nc.tensor.matmul(out=wb[:], lhsT=ones[:, 0:P], rhs=ones[:], start=True, stop=True)
+            for operand in operands:
+                nc.tensor.matmul(out=wb[:], lhsT=ones[:, 0:P], rhs=operand, start=True, stop=True)
 
         def spread_b1():
             bp = pso.tile([P, CH], F32, name="b1p", tag="ops")
@@ -327,17 +329,18 @@ def tile_embed_update_pa_kernel(tc, net_in, embeds, m, W1, b1, Wf, b_f, gamma, b
             elif has_b:
                 quantise(hc[gb][:], hs[gb][:], hgr[gb][:].rearrange("p r j -> p (r j)"))
             if i == -LEAD_A:
-                warm(5)
+                warm(ones[:], ones[:], trig[:], trig[:], w1r[0][:, 0, :], w1r[0][:, 0, :])
             if has_a:
                 for l in range(GROUPS[ga]):
                     transposes(first[ga] + l)
             if i == -LEAD_A:
-                warm(3)
+                warm(ones[:], w1r[1][:, 0, :], w1r[1][:, 0, :])
                 spread_b1()
             if has_a:
                 for l in range(GROUPS[ga]):
                     x_exit(ga, l)
                 if ga == 0:
+                    warm(xg[0][:, TOK * 4:TOK * 8], xg[0][:, TOK * 4:TOK * 8])
                     regroup_w1(nc.scalar.copy, 1, P - SHARE // 4, P)
                 quantise(xc[ga][:], xs[ga][:], xg[ga][:])
             if gb == 0:

from contextlib import ExitStack

import concourse.masks as masks
import concourse.mybir as mybir

F32 = mybir.dt.float32
BF16 = mybir.dt.bfloat16
U32 = mybir.dt.uint32
U8 = mybir.dt.uint8
I32 = mybir.dt.int32
FP8X4 = mybir.dt.float8_e4m3fn_x4
ACT = mybir.ActivationFunctionType
ALU = mybir.AluOpType
AX = mybir.AxisListType

P = 128
TOK = 128
LINKS = 16
IN = 1024
HID = 512
CH = 512
OUT = 511
LN_EPS = 1e-5
LINK_EPS = 1e-8
GROUPS = [2, 2, 2, 2, 2, 2, 2, 2]
NG = len(GROUPS)
LEAD_A = 4
LEAD_B = 2
BANKS = {"x": 2, "h": 2, "o": 4}
PINNED = True
SHARE = 128
GATE_COLS = 64

FLOPS = 2 * TOK * LINKS * IN * HID + 2 * TOK * LINKS * HID * CH


def tile_embed_update_pa_kernel(tc, net_in, embeds, m, W1, b1, Wf, b_f, gamma, beta, out):
    nc = tc.nc
    x2d = net_in.rearrange("b s k i -> (b s) (k i)")
    m2d = m.rearrange("b s k o -> (b s) (k o)")
    emb2d = embeds.rearrange("b s c -> (b s) c")
    out2d = out.rearrange("b s c -> (b s) c")
    w1v = W1.rearrange("(g u p e) c -> g p u (e c)", g=2, u=2, p=P, e=2)
    wfv = Wf.rearrange("(p t) c -> p t c", t=4, p=P)

    with ExitStack() as ctx:
        keep = ctx.enter_context(tc.tile_pool(name="keep", bufs=1))
        psx = ctx.enter_context(tc.psum_pool(name="psx", bufs=BANKS["x"]))
        psh = ctx.enter_context(tc.psum_pool(name="psh", bufs=BANKS["h"]))
        pso = ctx.enter_context(tc.psum_pool(name="pso", bufs=BANKS["o"]))
        if PINNED:
            ctx.enter_context(tc.manual_schedule())

        ident = keep.tile([P, P], F32, name="ident")
        masks.make_identity(nc, ident[:])
        vecs = keep.tile([P, 4 * CH], BF16, name="vecs")
        nc.vector.memset(vecs[:].bitcast(I32), 0)
        ones = keep.tile([P, CH], BF16, name="ones")
        nc.vector.memset(ones[:], 1.0)
        trig = keep.tile([P, CH], BF16, name="trig")
        nc.vector.memset(trig[:], 1.0)
        epsln = keep.tile([P, 1], F32, name="epsln")
        nc.vector.memset(epsln[:], LN_EPS)

        scr = keep.tile([P, 1], F32, name="scr")
        nc.scalar.activation(out=trig[:, 0:1], in_=epsln[:], func=ACT.Sigmoid)
        mbf = keep.tile([P, LINKS], BF16, name="mbf")
        w1r = [keep.tile([P, 4, HID], BF16, name="w1r%d" % g) for g in range(2)]
        wfr = keep.tile([P, 4, CH], BF16, name="wfr")
        xr = [keep.tile([P, 2 * IN], BF16, name="xr%d" % c) for c in range(LINKS // 2)]
        emb = keep.tile([P, OUT], BF16, name="emb")

        def load_w1(g):
            nc.sync.dma_start(out=w1r[g][:].rearrange("p (u e) c -> p u (e c)", u=2, e=2), in_=w1v[g])

        def load_x(c):
            nc.sync.dma_start(out=xr[c][:], in_=x2d[:, c * 2 * IN:(c + 1) * 2 * IN])

        load_w1(0)
        load_x(0)
        load_w1(1)
        nc.sync.dma_start(out=vecs[0:1, 3 * CH:4 * CH], in_=b1.unsqueeze(0))
        nc.sync.dma_start(out=vecs[0:1, 0:CH], in_=b_f.unsqueeze(0))
        load_x(1)
        nc.sync.dma_start(out=wfr[:], in_=wfv)
        load_x(2)
        nc.sync.dma_start(out=mbf[:], in_=m2d)
        load_x(3)
        load_x(4)
        load_x(5)
        load_x(6)
        load_x(7)
        nc.sync.dma_start(out=emb[:], in_=emb2d)
        nc.sync.dma_start(out=vecs[0:1, CH:CH + OUT], in_=gamma.unsqueeze(0))
        nc.sync.dma_start(out=vecs[0:1, 2 * CH:2 * CH + OUT], in_=beta.unsqueeze(0))

        b1f = keep.tile([P, 10], F32, name="b1f")
        mf = keep.tile([P, LINKS], F32, name="mf")
        msq = keep.tile([P, LINKS], F32, name="msq")
        mep = keep.tile([P, LINKS], F32, name="mep")
        w1c = keep.tile([P, 2 * HID], U32, name="w1c", align_bytes=256)
        w1s = keep.tile([P, 2 * HID], U8, name="w1s", align_bytes=256)
        w1g = [keep.tile([P, HID, 4], BF16, name="w1g%d" % g, align_bytes=64) for g in range(2)]
        wfc = keep.tile([P, CH], U32, name="wfc", align_bytes=256)
        wfs = keep.tile([P, CH], U8, name="wfs", align_bytes=256)
        wfg = keep.tile([P, CH, 4], BF16, name="wfg", align_bytes=64)
        first = [sum(GROUPS[:i]) for i in range(len(GROUPS))]
        xg, xc, xs, hpl, hgr, hc, hs = [], [], [], [], [], [], []
        for G, n in enumerate(GROUPS):
            xg.append(keep.tile([P, 2 * n * TOK * 4], BF16, name="xg%d" % G, align_bytes=64))
            xc.append(keep.tile([P, 2 * n * TOK], U32, name="xc%d" % G, align_bytes=256))
            xs.append(keep.tile([P, 2 * n * TOK], U8, name="xs%d" % G, align_bytes=256))
            hpl.append(keep.tile([P, 4, n * TOK], BF16, name="hpl%d" % G))
            hgr.append(keep.tile([P, n * TOK, 4], BF16, name="hgr%d" % G, align_bytes=64))
            hc.append(keep.tile([P, n * TOK], U32, name="hc%d" % G, align_bytes=256))
            hs.append(keep.tile([P, n * TOK], U8, name="hs%d" % G, align_bytes=256))
        sg = keep.tile([P, LINKS], F32, name="sg")
        st = keep.tile([P, LINKS], F32, name="st")
        acc = keep.tile([P, CH], F32, name="acc")
        gg = keep.tile([P, LINKS], F32, name="gg")
        gsum = keep.tile([P, 1], F32, name="gsum")
        lsum = keep.tile([P, 1], F32, name="lsum")
        lgsum = keep.tile([P, 1], F32, name="lgsum")
        wsum = keep.tile([P, 1], F32, name="wsum")
        lg = keep.tile([P, LINKS], F32, name="lg")
        wcopy = keep.tile([P, LINKS], F32, name="wcopy")
        banks = {}

        def regroup(copy, dst, src):
            copy(out=dst.rearrange("p (c i) t -> p c t i", i=8),
                 in_=src.rearrange("p t (c i) -> p c t i", i=8))

        def regroup_w1(copy, g, lo, hi):
            copy(out=w1g[g][:].rearrange("p (i c) t -> p c t i", i=4)[:, lo:hi, :, :],
                 in_=w1r[g][:].rearrange("p t (c i) -> p c t i", i=4)[:, lo:hi, :, :])

        def quantise(codes, scales, grouped):
            nc.vector.quantize_mx(out=codes.bitcast(FP8X4), scales=scales, in_=grouped)

        def small_prep():
            nc.vector.tensor_copy(out=mf[:], in_=mbf[:])
            nc.vector.tensor_tensor(out=msq[:], in0=mbf[:], in1=mbf[:], op=ALU.mult)
            nc.vector.tensor_scalar(out=mep[:], in0=mbf[:], scalar1=LINK_EPS, scalar2=None, op0=ALU.mult)

        def quantise_w1(g):
            quantise(w1c[:, g * HID:(g + 1) * HID], w1s[:, g * HID:(g + 1) * HID],
                     w1g[g][:].rearrange("p c t -> p (c t)"))

        def warm(*operands):
            wb = pso.tile([P, CH], F32, name="warmup", tag="ops")
            for operand in operands:
                nc.tensor.matmul(out=wb[:], lhsT=ones[:, 0:P], rhs=operand, start=True, stop=True)

        def spread_b1():
            bp = pso.tile([P, CH], F32, name="b1p", tag="ops")
            banks["b1"] = bp
            for j in range(4):
                nc.tensor.matmul(out=bp[:, 2 * j:2 * j + 2], lhsT=vecs[:, 3 * CH + j:4 * CH:4], rhs=ones[:, 0:2], start=True, stop=True)
            nc.tensor.matmul(out=bp[:, 8:10], lhsT=ones[:, 0:P], rhs=vecs[:, CH - 2:CH], start=True, stop=True)

        def transposes(k):
            words = xr[k // 2][:].bitcast(F32)
            xt = psx.tile([P, 4, TOK], F32, name="xt", tag="xt")
            banks["x%d" % k] = xt
            for w in range(4):
                lo = (k % 2) * (IN // 2) + w * P
                nc.tensor.transpose(out=xt[:, w, :], in_=words[:, lo:lo + P], identity=ident[:])

        def x_exit(G, l):
            n = GROUPS[G]
            dst = xg[G][:].bitcast(F32).rearrange("p (g l t u) -> p g l t u", g=2, l=n, t=TOK, u=2)
            xt = banks["x%d" % (first[G] + l)]
            nc.scalar.copy(out=dst[:, :, l, :, :], in_=xt[:].rearrange("p (g u) t -> p g t u", g=2, u=2))

        def stage1(G, b):
            n = GROUPS[G]
            w = n * TOK
            per = 4 // n
            hp = psh.tile([P, per, w], F32, name="hp", tag="hp")
            banks["h%d_%d" % (G, b)] = hp
            for jj in range(per):
                j = b * per + jj
                for g in range(2):
                    lo = g * HID + j * P
                    nc.tensor.matmul_mx(out=hp[:, jj, :],
                                        lhsT=w1c[:, lo:lo + P].bitcast(FP8X4), lhsT_scale=w1s[:, lo:lo + P],
                                        rhs=xc[G][:, g * w:(g + 1) * w].bitcast(FP8X4),
                                        rhs_scale=xs[G][:, g * w:(g + 1) * w],
                                        start=(g == 0), stop=(g == 1))

        def h_exit(G, j):
            per = 4 // GROUPS[G]
            hp = banks["h%d_%d" % (G, j // per)]
            nc.scalar.activation(out=hpl[G][:, j, :], in_=hp[:, j % per, :], func=ACT.Relu,
                                 bias=b1f[:, 2 * j:2 * j + 1], scale=1.0)

        def stage2(G, l):
            op = pso.tile([P, CH], F32, name="op", tag="ops")
            banks["o%d" % (first[G] + l)] = op
            nc.tensor.matmul_mx(out=op[:],
                                lhsT=hc[G][:, l * TOK:(l + 1) * TOK].bitcast(FP8X4),
                                lhsT_scale=hs[G][:, l * TOK:(l + 1) * TOK],
                                rhs=wfc[:].bitcast(FP8X4), rhs_scale=wfs[:], start=True, stop=True)

        def gate(k):
            nc.scalar.activation(out=sg[:, k:k + 1], in_=banks["o%d" % k][:, OUT:CH], func=ACT.Sigmoid,
                                 bias=b1f[:, 9:10], scale=1.0)

        def early_gate(l):
            G = NG - 1
            k = first[G] + l
            gl = psx.tile([P, GATE_COLS], F32, name="gl", tag="xt")
            nc.tensor.matmul_mx(out=gl[:],
                                lhsT=hc[G][:, l * TOK:(l + 1) * TOK].bitcast(FP8X4),
                                lhsT_scale=hs[G][:, l * TOK:(l + 1) * TOK],
                                rhs=wfc[:, CH - GATE_COLS:CH].bitcast(FP8X4),
                                rhs_scale=wfs[:, CH - GATE_COLS:CH], start=True, stop=True)
            nc.scalar.activation(out=sg[:, k:k + 1], in_=gl[:, GATE_COLS - 1:GATE_COLS], func=ACT.Sigmoid,
                                 bias=b1f[:, 9:10], scale=1.0)
            weight(k)

        def weight(k):
            nc.scalar.activation(out=st[:, k:k + 1], in_=sg[:, k:k + 1], func=ACT.Identity,
                                 bias=mep[:, k:k + 1], scale=msq[:, k:k + 1])

        def step_l():
            nc.vector.tensor_scalar(out=lsum[:], in0=gsum[:], scalar1=LINKS * LINK_EPS, scalar2=None, op0=ALU.add)
            nc.vector.scalar_tensor_tensor(out=lg[:], in0=gg[:], scalar=LINK_EPS, in1=gg[:],
                                           op0=ALU.add, op1=ALU.mult, accum_out=lgsum[:])

        def regroup_last(copy, l):
            G = NG - 1
            cols = slice(l * TOK, (l + 1) * TOK)
            regroup(copy, hgr[G][:, cols, :], hpl[G][:, :, cols])

        def quantise_last(l):
            G = NG - 1
            cols = slice(l * TOK, (l + 1) * TOK)
            quantise(hc[G][:, cols], hs[G][:, cols], hgr[G][:, cols, :].rearrange("p r j -> p (r j)"))

        def step_q():
            quantise_last(0)

        def step_sc():
            nc.vector.tensor_scalar(out=sc[:], in0=lgsum[:], scalar1=rl[:, 0:1], scalar2=rl[:, 0:1],
                                    op0=ALU.mult, op1=ALU.mult)

        def pool_link(k, woven=None):
            op = banks["o%d" % k]
            for lo, hi in [(0, OUT)] if k < 11 else halves:
                if woven is not None and lo > 0:
                    woven()
                if k == 0:
                    nc.vector.tensor_scalar(out=acc[:, lo:hi], in0=op[:, lo:hi],
                                            scalar1=st[:, k:k + 1], scalar2=None, op0=ALU.mult)
                else:
                    nc.vector.scalar_tensor_tensor(out=acc[:, lo:hi], in0=op[:, lo:hi],
                                                   scalar=st[:, k:k + 1], in1=acc[:, lo:hi],
                                                   op0=ALU.mult, op1=ALU.add)

        halves = [(0, 256), (256, OUT)]
        sacc = keep.tile([P, 2], F32, name="sacc")
        nmu0 = keep.tile([P, 1], F32, name="nmu0")
        nes = keep.tile([P, 1], F32, name="nes")
        scr2 = keep.tile([P, CH], F32, name="scr2")
        rl = keep.tile([P, 1], F32, name="rl")
        sc = keep.tile([P, 1], F32, name="sc")
        nsc = keep.tile([P, 1], F32, name="nsc")

        for i in range(-LEAD_A, NG):
            ga, gb, gc = i + LEAD_A, i + LEAD_B, i
            has_a, has_b, has_c = ga < NG, 0 <= gb < NG, gc >= 0
            last = i == NG - 1
            if i == -LEAD_A:
                regroup_w1(nc.vector.tensor_copy, 0, 0, P)
                quantise_w1(0)
                regroup_w1(nc.vector.tensor_copy, 1, 0, P - SHARE // 4)
            if i == 1 - LEAD_A:
                nc.vector.tensor_copy(out=b1f[:], in_=banks["b1"][:, 0:10])
                regroup(nc.vector.tensor_copy, wfg[:, 0:CH // 2, :], wfr[:, :, 0:CH // 2])
            if has_c and not last:
                for l in range(GROUPS[gc]):
                    stage2(gc, l)
                if not last:
                    for l in range(GROUPS[gc]):
                        gate(first[gc] + l)
                    for l in range(GROUPS[gc]):
                        weight(first[gc] + l)
                if gc == NG - 2:
                    for l in range(2):
                        early_gate(l)
                        stage2(NG - 1, l)
                    nc.scalar.activation(out=wcopy[:], in_=st[:], func=ACT.Copy, accum_out=wsum[:])
                    nc.scalar.activation(out=scr2[:, 0:OUT], in_=emb[:], func=ACT.Copy, scale=-1.0 / OUT,
                                         accum_out=nes[:, 0:1])
                    bfp = psh.tile([P, CH], F32, name="bfp", tag="hp")
                    nc.tensor.matmul(out=bfp[:], lhsT=ones[:, 0:P], rhs=vecs[:, 0:CH], start=True, stop=True)
            if has_b:
                for b in range(GROUPS[gb]):
                    stage1(gb, b)
                for j in range(4):
                    h_exit(gb, j)
            if last:
                nc.vector.scalar_tensor_tensor(out=gg[:], in0=sg[:], scalar=1.0, in1=mf[:],
                                               op0=ALU.mult, op1=ALU.mult, accum_out=gsum[:])
            if has_c:
                pool_link(first[gc], step_l if last else None)
            if last:
                nc.vector.reciprocal(out=rl[:], in_=lsum[:])
            if has_c and gb == NG - 1:
                regroup_last(nc.vector.tensor_copy, 0)
                regroup_last(nc.scalar.copy, 1)
            elif has_b:
                regroup(nc.vector.tensor_copy, hgr[gb][:], hpl[gb][:])
            if has_c:
                pool_link(first[gc] + 1, step_sc if last else step_q if gb == NG - 1 else None)
            if last:
                nc.vector.tensor_scalar(out=nsc[:], in0=sc[:], scalar1=-1.0 / OUT, scalar2=None, op0=ALU.mult)
                for h, (lo, hi) in enumerate(halves):
                    nc.vector.scalar_tensor_tensor(out=acc[:, lo:hi], in0=bfp[:, lo:hi], scalar=wsum[:, 0:1],
                                                   in1=acc[:, lo:hi], op0=ALU.mult, op1=ALU.add,
                                                   accum_out=sacc[:, h:h + 1])
                nc.vector.tensor_scalar(out=nmu0[:], in0=sacc[:, 0:1], scalar1=nsc[:, 0:1], scalar2=nes[:, 0:1],
                                        op0=ALU.mult, op1=ALU.add)
            if gb == 0:
                quantise(wfc[:], wfs[:], wfg[:].rearrange("p c t -> p (c t)"))
            if has_c and gb == NG - 1:
                quantise_last(1)
            elif has_b:
                quantise(hc[gb][:], hs[gb][:], hgr[gb][:].rearrange("p r j -> p (r j)"))
            if i == -LEAD_A:
                warm(ones[:], ones[:], trig[:], trig[:], w1r[0][:, 0, :], w1r[0][:, 0, :])
            if has_a:
                for l in range(GROUPS[ga]):
                    transposes(first[ga] + l)
            if i == -LEAD_A:
                warm(ones[:], w1r[1][:, 0, :], w1r[1][:, 0, :])
                spread_b1()
            if has_a:
                for l in range(GROUPS[ga]):
                    x_exit(ga, l)
                if ga == 0:
                    warm(xg[0][:, TOK * 4:TOK * 8], xg[0][:, TOK * 4:TOK * 8])
                    regroup_w1(nc.scalar.copy, 1, P - SHARE // 4, P)
                quantise(xc[ga][:], xs[ga][:], xg[ga][:])
            if gb == 0:
                small_prep()
            if i == -LEAD_A:
                quantise_w1(1)
            if i == 1 - LEAD_A:
                regroup(nc.vector.tensor_copy, wfg[:, CH // 2:CH, :], wfr[:, :, CH // 2:CH])

        nc.scalar.activation(out=scr[:], in_=sg[:, LINKS - 1:LINKS], func=ACT.Abs_reciprocal_sqrt,
                             bias=epsln[:, 0:1], scale=1.0)
        gam = psx.tile([P, CH], F32, name="gam", tag="xt")
        nc.tensor.matmul(out=gam[:], lhsT=ones[:, 0:P], rhs=vecs[:, CH:2 * CH], start=True, stop=True)
        bet = psx.tile([P, CH], F32, name="bet", tag="xt")
        nc.tensor.matmul(out=bet[:], lhsT=ones[:, 0:P], rhs=vecs[:, 2 * CH:3 * CH], start=True, stop=True)

        ee = keep.tile([P, CH], F32, name="ee")
        negmu = keep.tile([P, 1], F32, name="negmu")
        vs = keep.tile([P, 2], F32, name="vs")
        vt = keep.tile([P, 1], F32, name="vt")
        rstd = keep.tile([P, 1], F32, name="rstd")
        y1 = keep.tile([P, CH], F32, name="y1")
        yy = keep.tile([P, CH], F32, name="yy")

        def residual(lo, hi):
            nc.vector.scalar_tensor_tensor(out=ee[:, lo:hi], in0=acc[:, lo:hi], scalar=sc[:, 0:1],
                                           in1=emb[:, lo:hi], op0=ALU.mult, op1=ALU.add)

        residual(*halves[0])
        nc.vector.tensor_scalar(out=negmu[:], in0=sacc[:, 1:2], scalar1=nsc[:, 0:1], scalar2=nmu0[:, 0:1],
                                op0=ALU.mult, op1=ALU.add)
        residual(*halves[1])
        for h, (lo, hi) in enumerate(halves):
            nc.scalar.activation(out=scr2[:, lo:hi], in_=ee[:, lo:hi], func=ACT.Square,
                                 bias=negmu[:, 0:1], scale=1.0, accum_out=vs[:, h:h + 1])
        nc.scalar.activation(out=vt[:], in_=vs[:, 0:1], func=ACT.Identity,
                             bias=epsln[:, 0:1], scale=1.0 / OUT)
        nc.scalar.activation(out=rstd[:], in_=vs[:, 1:2], func=ACT.Abs_reciprocal_sqrt,
                             bias=vt[:, 0:1], scale=1.0 / OUT)
        for lo, hi in halves:
            nc.vector.scalar_tensor_tensor(out=y1[:, lo:hi], in0=ee[:, lo:hi], scalar=negmu[:, 0:1],
                                           in1=gam[:, lo:hi], op0=ALU.add, op1=ALU.mult)
        for lo, hi in halves:
            nc.vector.scalar_tensor_tensor(out=yy[:, lo:hi], in0=y1[:, lo:hi], scalar=rstd[:, 0:1],
                                           in1=bet[:, lo:hi], op0=ALU.mult, op1=ALU.add)
            nc.sync.dma_start(out=out2d[:, lo:hi], in_=yy[:, lo:hi])
